import numpy as np
import ml_dtypes


def mxq(x, axis, fmt="e4m3"):
    dtype, down = {"e4m3": (ml_dtypes.float8_e4m3fn, 7), "e5m2": (ml_dtypes.float8_e5m2, 14)}[fmt]
    v = np.moveaxis(np.asarray(x, np.float32).astype(ml_dtypes.bfloat16).astype(np.float64), axis, -1)
    blocks = v.reshape(v.shape[:-1] + (-1, 32))
    amax = np.abs(blocks).max(-1, keepdims=True)
    byte = np.maximum(np.where(amax > 0, np.frexp(amax)[1] - 1 + 127, 0) - down, 1)
    scale = np.exp2(byte - 127.0)
    codes = (blocks / scale).astype(np.float32).astype(dtype).astype(np.float64)
    return np.moveaxis((codes * scale).reshape(v.shape), -1, axis)


WIDE = False


def mx_kscale(k):
    if not WIDE:
        return np.ones(k)
    levels = np.array([10, -10, 5, -5, 0])
    a = np.random.permutation(np.resize(levels, k // 512 * 4)).reshape(k // 512, 4)
    idx = np.arange(k)
    return np.exp2(a[idx // 512, idx % 128 // 32])


BF16 = ml_dtypes.bfloat16


def bf(x):
    return np.asarray(x, np.float32).astype(BF16)


def f64(x):
    return np.asarray(x).astype(np.float64)


E2M1 = np.array([0.0, 0.5, 1.0, 1.5, 2.0, 3.0, 4.0, 6.0, -0.0, -0.5, -1.0, -1.5, -2.0, -3.0, -4.0, -6.0])


def pack_weight(w, fmt):
    k, n = w.shape
    w = f64(bf(w)).reshape(k // 32, 32, n)
    amax = np.abs(w).max(1)
    if fmt == "e4m3":
        byte = np.frexp(amax)[1] - 1 + 127 - 7
    else:
        mant, ex = np.frexp(amax / 6.0)
        byte = np.where(mant > 0.5, ex, ex - 1) + 127
    byte = np.clip(np.where(amax > 0, byte, 1), 1, 254)
    scaled = (w * np.exp2(127.0 - byte)[:, None, :]).reshape(k, n).astype(np.float32)
    by_word = np.ascontiguousarray(scaled.reshape(k // 512, 128, 4, n).transpose(0, 1, 3, 2))
    if fmt == "e4m3":
        words = by_word.astype(ml_dtypes.float8_e4m3fn).view(np.uint8)
    else:
        c = by_word.astype(ml_dtypes.float4_e2m1fn).view(np.uint8) & 0xF
        words = c[..., 0::2] | (c[..., 1::2] << 4)
    return np.ascontiguousarray(words), np.ascontiguousarray(byte.astype(np.uint8).reshape(k // 512, 16, n))


def unpack_weight(words, scales, fmt):
    g, p, n, _ = words.shape
    if fmt == "e4m3":
        vals = np.ascontiguousarray(words).view(ml_dtypes.float8_e4m3fn).astype(np.float64)
    else:
        nib = np.empty((g, p, n, 4), np.uint8)
        nib[..., 0::2] = words & 0xF
        nib[..., 1::2] = words >> 4
        vals = E2M1[nib]
    vals = vals * np.repeat(np.exp2(scales.astype(np.float64) - 127.0), 8, axis=1)[..., None]
    return vals.transpose(0, 1, 3, 2).reshape(g * 512, n)


B, C, H, W, P, DIM = 16, 8, 256, 256, 16, 512
SHIFT = P // 2
WD = 5 * C * P * P // 4
N = (H // P) * (W // P)
EPS = 1e-5
XS = 0.015
FMT = "e4m3"


def patch_shift(x, shift):
    xp = np.pad(x, ((0, 0), (0, 0), (shift, shift), (shift, shift)))
    s2 = 2 * shift
    return np.concatenate([x, xp[:, :, :-s2, :-s2], xp[:, :, :-s2, s2:], xp[:, :, s2:, :-s2], xp[:, :, s2:, s2:]], axis=1)


def haar_detail_mean(x):
    b_, c_, h, w = x.shape
    r = x.reshape(b_, c_, h // 2, 2, w // 2, 2)
    return (3.0 * r[:, :, :, 0, :, 0] - r[:, :, :, 0, :, 1] - r[:, :, :, 1, :, 0] - r[:, :, :, 1, :, 1]) / 6.0


def patchify(x, p):
    b_, c_, hh, ww = x.shape
    h, w = hh // p, ww // p
    return x.reshape(b_, c_, h, p, w, p).transpose(0, 2, 4, 3, 5, 1).reshape(b_, h * w, p * p * c_)


def layernorm(u, g, b):
    m = u.mean(-1, keepdims=True)
    v = np.square(u - m).mean(-1, keepdims=True)
    return (u - m) / np.sqrt(v + EPS) * g + b


def setup_inputs():
    s = mx_kscale(WD)
    x = bf(np.random.standard_normal((B, C, H, W)) * XS)
    ln2_g = bf((1.0 + 0.1 * np.random.standard_normal(WD)) * s)
    ln2_b = bf(0.1 * np.random.standard_normal(WD) * s)
    w2_words, w2_scales = pack_weight(np.random.standard_normal((WD, DIM)) / np.sqrt(WD) / s[:, None], FMT)
    b2 = bf(0.3 * np.random.standard_normal(DIM))
    tok = bf(np.random.standard_normal((B, N, DIM)))
    return {"x": x,
            "ln2_g": ln2_g,
            "ln2_b": ln2_b,
            "w2_words": w2_words,
            "w2_scales": w2_scales,
            "b2": b2,
            "tok": tok}


def reference(x, ln2_g, ln2_b, w2_words, w2_scales, b2, tok):
    waves = haar_detail_mean(patch_shift(f64(x), SHIFT))
    z = layernorm(patchify(waves, P // 2), f64(ln2_g), f64(ln2_b))
    wtok = (mxq(z, 2, "e4m3") @ unpack_weight(w2_words, w2_scales, FMT)) + f64(b2)
    return f64(tok) + wtok

@@ -1,0 +1,291 @@
+from contextlib import ExitStack
+
+import concourse.mybir as mybir
+from concourse.masks import make_identity
+
+F32 = mybir.dt.float32
+BF16 = mybir.dt.bfloat16
+U32 = mybir.dt.uint32
+U8 = mybir.dt.uint8
+I32 = mybir.dt.int32
+FP8X4 = mybir.dt.float8_e4m3fn_x4
+ALU = mybir.AluOpType
+ACT = mybir.ActivationFunctionType
+
+P = 128
+BATCH = 16
+DIM = 512
+K = 2560
+PASSES = K // 512
+EPS = 1e-5
+PLANES = 4
+BAND_ROWS = 8
+BANDS = 5
+PADDED = 136
+TOKEN_ROWS = 4
+GROUP = 4
+GROUPS = 16 // GROUP
+WORDS = K // 2
+
+FLOPS = 2 * BATCH * 256 * K * DIM
+
+
+def tile_shiftedpatchtokenization_pb_t_kernel(tc, x, ln2_g, ln2_b, w2_words, w2_scales, b2, tok, out):
+    nc = tc.nc
+    with ExitStack() as ctx:
+        const = ctx.enter_context(tc.tile_pool(name="const", bufs=1))
+        x_pool = ctx.enter_context(tc.tile_pool(name="x_pool", bufs=6))
+        band_pool = ctx.enter_context(tc.tile_pool(name="band_pool", bufs=3))
+        haar_pool = ctx.enter_context(tc.tile_pool(name="haar_pool", bufs=2))
+        stat_pool = ctx.enter_context(tc.tile_pool(name="stat_pool", bufs=2))
+        u_pool = ctx.enter_context(tc.tile_pool(name="u_pool", bufs=2))
+        z_pool = ctx.enter_context(tc.tile_pool(name="z_pool", bufs=3))
+        code_pool = ctx.enter_context(tc.tile_pool(name="code_pool", bufs=2))
+        io_pool = ctx.enter_context(tc.tile_pool(name="io_pool", bufs=4))
+        psum_t = ctx.enter_context(tc.psum_pool(name="psum_t", bufs=4))
+        psum_mx = ctx.enter_context(tc.psum_pool(name="psum_mx", bufs=2))
+        psum_stat = ctx.enter_context(tc.psum_pool(name="psum_stat", bufs=1))
+
+        x_body = x.rearrange("b c (q r) w -> b (c q) (r w)", q=4)
+        x_plane = x.rearrange("b (l c) h w -> l b c (h w)", c=2)
+        tok_rows = tok.rearrange("b t n -> (b t) n").rearrange("(m s) n -> m s n", s=64)
+        out_rows = out.rearrange("b t n -> (b t) n").rearrange("(m s) n -> m s n", s=64)
+
+        ident = const.tile([P, P], F32)
+        make_identity(nc, ident[:])
+        ident_bcq = ident[:].rearrange("p (b c q) -> p b c q", b=BATCH, c=2, q=4)
+        perm = const.tile([P, P], F32)
+        nc.vector.tensor_copy(
+            out=perm[:].rearrange("p (c b q) -> p c b q", c=2, b=BATCH, q=4),
+            in_=ident[:].rearrange("p (b c q) -> p c b q", b=BATCH, c=2, q=4),
+        )
+        pair = const.tile([P, P], F32)
+        pair_bcq = pair[:].rearrange("p (b c q) -> p b c q", b=BATCH, c=2, q=4)
+        nc.vector.tensor_copy(out=pair_bcq[:, :, 0, :], in_=ident_bcq[:, :, 1, :])
+        nc.vector.tensor_copy(out=pair_bcq[:, :, 1, :], in_=ident_bcq[:, :, 0, :])
+        nc.vector.tensor_tensor(out=pair[:], in0=pair[:], in1=ident[:], op=ALU.add)
+
+        gain_bf = const.tile([P, PASSES, 4], BF16)
+        bias_bf = const.tile([P, PASSES, 4], BF16)
+        nc.sync.dma_start(out=gain_bf[:], in_=ln2_g.rearrange("(g p t) -> p g t", g=PASSES, p=P, t=4))
+        nc.sync.dma_start(out=bias_bf[:], in_=ln2_b.rearrange("(g p t) -> p g t", g=PASSES, p=P, t=4))
+        gain = const.tile([P, PASSES, 4], F32)
+        bias = const.tile([P, PASSES, 4], F32)
+        nc.vector.tensor_copy(out=gain[:], in_=gain_bf[:])
+        nc.vector.tensor_copy(out=bias[:], in_=bias_bf[:])
+
+        quad_sums = const.tile([P, 2, 2 * BANDS, 34], F32)
+        nc.vector.memset(quad_sums[:], 0.0)
+
+        w_codes = const.tile([P, PASSES, DIM], U32, align_bytes=64)
+        w_scales = const.tile([P, PASSES, DIM], U8, align_bytes=64)
+        b2_all = const.tile([P, DIM], BF16)
+
+        def load_weights():
+            nc.vector.memset(w_scales[:].bitcast(I32), 0)
+            for quadrant in range(4):
+                nc.sync.dma_start(
+                    out=w_scales[32 * quadrant : 32 * quadrant + 4, :, :].bitcast(I32),
+                    in_=w2_scales[:, 4 * quadrant : 4 * quadrant + 4, :].rearrange("g r n -> r g n").bitcast(I32),
+                )
+            nc.sync.dma_start(
+                out=w_codes[:].bitcast(I32),
+                in_=w2_words.rearrange("g p n t -> p g (n t)").bitcast(I32),
+            )
+            nc.sync.dma_start(out=b2_all[:], in_=b2.partition_broadcast(P))
+
+        bands = []
+
+        def haar_band(kb):
+            band = band_pool.tile([P, PLANES, BAND_ROWS, PADDED], F32, name="band")
+            bands.append(band)
+            nc.vector.memset(band[:, :, :, 0:4], 0.0)
+            nc.vector.memset(band[:, :, :, PADDED - 4 : PADDED], 0.0)
+            for l in range(PLANES):
+                xt = x_pool.tile([P, 2 * BAND_ROWS, 256], BF16, name="xt")
+                first = 16 * kb - 8
+                lo = max(first, 0)
+                hi = min(first + 16, 64)
+                if kb == 0:
+                    nc.vector.memset(xt[:, 0:8, :], 0.0)
+                    for q in range(1, 4):
+                        nc.sync.dma_start(
+                            out=xt[q:P:4, 0:8, :].rearrange("p r w -> p (r w)"),
+                            in_=x_plane[l][:, :, (64 * q - 8) * 256 : 64 * q * 256],
+                        )
+                if kb == BANDS - 1:
+                    nc.vector.memset(xt[:, 8:16, :], 0.0)
+                    for q in range(0, 3):
+                        nc.sync.dma_start(
+                            out=xt[q:P:4, 8:16, :].rearrange("p r w -> p (r w)"),
+                            in_=x_plane[l][:, :, (64 * q + 64) * 256 : (64 * q + 72) * 256],
+                        )
+                nc.sync.dma_start(
+                    out=xt[:, lo - first : hi - first, :].rearrange("p r w -> p (r w)"),
+                    in_=x_body[:, 8 * l : 8 * l + 8, lo * 256 : hi * 256],
+                )
+                blocks = xt[:].rearrange("p (r v) (w h) -> p r v w h", v=2, h=2)
+                rest = haar_pool.tile([P, BAND_ROWS, 128], F32, name="rest")
+                nc.vector.tensor_tensor(out=rest[:], in0=blocks[:, :, 1, :, 0], in1=blocks[:, :, 1, :, 1], op=ALU.add)
+                nc.vector.tensor_tensor(out=rest[:], in0=rest[:], in1=blocks[:, :, 0, :, 1], op=ALU.add)
+                nc.vector.scalar_tensor_tensor(
+                    out=band[:, l, :, 4 : PADDED - 4],
+                    in0=blocks[:, :, 0, :, 0],
+                    scalar=3.0,
+                    in1=rest[:],
+                    op0=ALU.mult,
+                    op1=ALU.subtract,
+                )
+            bn = stat_pool.tile([P, 2, 32, 6], F32, name="bn")
+            for yq in range(2):
+                for xq in range(32):
+                    nc.vector.bn_stats(
+                        out=bn[:, yq, xq, :],
+                        in_=band[:, :, 4 * yq : 4 * yq + 4, 4 + 4 * xq : 8 + 4 * xq],
+                    )
+            squares = stat_pool.tile([P, 2, 32, 2], F32, name="squares")
+            nc.vector.tensor_tensor(out=squares[:], in0=bn[:, :, :, 1:6:3], in1=bn[:, :, :, 1:6:3], op=ALU.mult)
+            nc.vector.scalar_tensor_tensor(
+                out=squares[:], in0=squares[:], scalar=32.0, in1=bn[:, :, :, 2:6:3], op0=ALU.mult, op1=ALU.add
+            )
+            rows = slice(2 * kb, 2 * kb + 2)
+            nc.vector.tensor_tensor(out=quad_sums[:, 0, rows, 1:33], in0=bn[:, :, :, 1], in1=bn[:, :, :, 4], op=ALU.add)
+            nc.vector.tensor_tensor(
+                out=quad_sums[:, 1, rows, 1:33], in0=squares[:, :, :, 0], in1=squares[:, :, :, 1], op=ALU.add
+            )
+
+        def token_stats(i):
+            inner = stat_pool.tile([P, 2, 34], F32, name="inner")
+            outer = stat_pool.tile([P, 2, 34], F32, name="outer")
+            nc.vector.tensor_tensor(
+                out=inner[:], in0=quad_sums[:, :, 2 * i + 1, :], in1=quad_sums[:, :, 2 * i + 2, :], op=ALU.add
+            )
+            nc.vector.tensor_tensor(
+                out=outer[:], in0=quad_sums[:, :, 2 * i, :], in1=quad_sums[:, :, 2 * i + 3, :], op=ALU.add
+            )
+            nc.vector.tensor_tensor(out=outer[:], in0=outer[:], in1=inner[:], op=ALU.add)
+            nc.vector.tensor_tensor(out=inner[:], in0=inner[:], in1=outer[:], op=ALU.add)
+            sums = stat_pool.tile([P, 2, 16], F32, name="sums")
+            edge = stat_pool.tile([P, 2, 16], F32, name="edge")
+            nc.vector.tensor_tensor(out=sums[:], in0=inner[:, :, 1:33:2], in1=inner[:, :, 2:34:2], op=ALU.add)
+            nc.vector.tensor_tensor(out=edge[:], in0=outer[:, :, 0:32:2], in1=outer[:, :, 3:34:2], op=ALU.add)
+            nc.vector.tensor_tensor(out=sums[:], in0=sums[:], in1=edge[:], op=ALU.add)
+            both = psum_stat.tile([P, 32], F32, name="both")
+            nc.tensor.matmul(out=both[:], lhsT=pair[:], rhs=sums[:].rearrange("p s j -> p (s j)"), start=True, stop=True)
+            mean = stat_pool.tile([P, 16], F32, name="mean")
+            var = stat_pool.tile([P, 16], F32, name="var")
+            mean_sq = stat_pool.tile([P, 16], F32, name="mean_sq")
+            std = stat_pool.tile([P, 16], F32, name="std")
+            rstd = stat_pool.tile([P, 16], F32, name="rstd")
+            shift = stat_pool.tile([P, 16], F32, name="shift")
+            nc.vector.tensor_scalar(out=mean[:], in0=both[:, 0:16], scalar1=32.0 / K, scalar2=None, op0=ALU.mult)
+            nc.vector.tensor_scalar(
+                out=var[:], in0=both[:, 16:32], scalar1=1.0 / K, scalar2=36.0 * EPS, op0=ALU.mult, op1=ALU.add
+            )
+            nc.vector.tensor_tensor(out=mean_sq[:], in0=mean[:], in1=mean[:], op=ALU.mult)
+            nc.vector.tensor_tensor(out=var[:], in0=var[:], in1=mean_sq[:], op=ALU.subtract)
+            nc.scalar.activation(out=std[:], in_=var[:], func=ACT.Sqrt)
+            nc.vector.reciprocal(out=rstd[:], in_=std[:])
+            nc.vector.scalar_tensor_tensor(
+                out=shift[:], in0=mean[:], scalar=-1.0, in1=rstd[:], op0=ALU.mult, op1=ALU.mult
+            )
+            return mean, rstd, shift
+
+        def normalise(dst, src, stats, j, on_vector):
+            mean, rstd, shift = stats
+            if on_vector:
+                nc.vector.tensor_scalar(
+                    out=dst, in0=src, scalar1=mean[:, j : j + 1], scalar2=rstd[:, j : j + 1],
+                    op0=ALU.subtract, op1=ALU.mult,
+                )
+            else:
+                nc.scalar.activation(
+                    out=dst, in_=src, func=ACT.Identity, bias=shift[:, j : j + 1], scale=rstd[:, j : j + 1]
+                )
+
+        def patch_group(i, jc, stats):
+            upper = bands[i]
+            lower = bands[i + 1]
+            tok_tiles = []
+            for jp in range(2):
+                s0 = 16 * i + GROUP * jc + 2 * jp
+                tok_bf = io_pool.tile([P, DIM], BF16, name="tok_bf")
+                nc.sync.dma_start(out=tok_bf[:], in_=tok_rows[:, s0 : s0 + 2, :])
+                tok_b2 = io_pool.tile([P, DIM], F32, name="tok_b2")
+                nc.gpsimd.tensor_tensor(out=tok_b2[:], in0=tok_bf[:], in1=b2_all[:], op=ALU.add)
+                tok_tiles.append(tok_b2)
+
+            u = u_pool.tile([P, GROUP, WORDS], F32, name="u")
+            for jl in range(GROUP):
+                j = GROUP * jc + jl
+                on_vector = jl == GROUP - 1
+                uv = u[:, jl, :].rearrange("p (a b c l) -> p a b c l", a=8, b=8, c=5, l=PLANES)
+                x0 = 8 * j
+                normalise(
+                    uv[:, 0:4, :, 0, :], upper[:, :, 4:8, x0 + 4 : x0 + 12].rearrange("p l a b -> p a b l"),
+                    stats, j, on_vector,
+                )
+                normalise(
+                    uv[:, 4:8, :, 0, :], lower[:, :, 0:4, x0 + 4 : x0 + 12].rearrange("p l a b -> p a b l"),
+                    stats, j, on_vector,
+                )
+                for sy, band in enumerate((upper, lower)):
+                    for sx in range(2):
+                        normalise(
+                            uv[:, :, :, 1 + 2 * sy + sx, :],
+                            band[:, :, :, x0 + 8 * sx : x0 + 8 * sx + 8].rearrange("p l a b -> p a b l"),
+                            stats, j, on_vector,
+                        )
+
+            z_codes = code_pool.tile([P, PASSES, GROUP * 64], U32, name="z_codes", align_bytes=64)
+            z_scales = code_pool.tile([P, PASSES, GROUP * 64], U8, name="z_scales", align_bytes=64)
+            for g in range(PASSES):
+                planes = z_pool.tile([P, 4, GROUP * 64], BF16, name="planes")
+                for ca in range(2):
+                    turned = psum_t.tile([P, GROUP, P], F32, name="turned")
+                    for jl in range(GROUP):
+                        nc.tensor.transpose(
+                            out=turned[:, jl, :], in_=u[:, jl, 256 * g + ca : 256 * (g + 1) : 2], identity=perm[:]
+                        )
+                    for cb in range(2):
+                        t = 2 * ca + cb
+                        nc.scalar.activation(
+                            out=planes[:, t, :].rearrange("p (jp m jj) -> p jp m jj", jp=2, m=64, jj=2),
+                            in_=turned[:, :, 64 * cb : 64 * cb + 64].rearrange("p (jp jj) m -> p jp m jj", jj=2),
+                            func=ACT.Identity,
+                            bias=bias[:, g, t : t + 1],
+                            scale=gain[:, g, t : t + 1],
+                        )
+                grouped = z_pool.tile([P, 4 * GROUP * 64], BF16, name="grouped", align_bytes=64)
+                nc.vector.tensor_copy(
+                    out=grouped[:].rearrange("p (w t) -> p w t", t=4), in_=planes[:].rearrange("p t w -> p w t")
+                )
+                nc.vector.quantize_mx(out=z_codes[:, g, :].bitcast(FP8X4), scales=z_scales[:, g, :], in_=grouped[:])
+
+            for jp in range(2):
+                s0 = 16 * i + GROUP * jc + 2 * jp
+                cols = slice(P * jp, P * jp + P)
+                acc = psum_mx.tile([P, DIM], F32, name="acc")
+                for g in range(PASSES):
+                    nc.tensor.matmul_mx(
+                        out=acc[:],
+                        lhsT=z_codes[:, g, cols].bitcast(FP8X4),
+                        lhsT_scale=z_scales[:, g, cols],
+                        rhs=w_codes[:, g, :].bitcast(FP8X4),
+                        rhs_scale=w_scales[:, g, :],
+                        start=(g == 0),
+                        stop=(g == PASSES - 1),
+                    )
+                result = io_pool.tile([P, DIM], F32, name="result")
+                nc.vector.tensor_tensor(out=result[:], in0=acc[:], in1=tok_tiles[jp][:], op=ALU.add)
+                nc.sync.dma_start(out=out_rows[:, s0 : s0 + 2, :], in_=result[:])
+
+        haar_band(0)
+        haar_band(1)
+        load_weights()
+        for i in range(TOKEN_ROWS):
+            stats = token_stats(i)
+            if i + 2 < BANDS:
+                haar_band(i + 2)
+            for jc in range(GROUPS):
+                patch_group(i, jc, stats)

@@ -22,10 +22,12 @@ PLANES = 4
 BAND_ROWS = 8
 BANDS = 5
 PADDED = 136
+QUAD_PITCH = 36
 TOKEN_ROWS = 4
 GROUP = 4
 GROUPS = 16 // GROUP
 WORDS = K // 2
+VECTOR_PATCHES = (1, 1, 3, 3)
 
 FLOPS = 2 * BATCH * 256 * K * DIM
 
@@ -35,7 +37,7 @@ def tile_shiftedpatchtokenization_pb_t_kernel(tc, x, ln2_g, ln2_b, w2_words, w2_
     with ExitStack() as ctx:
         const = ctx.enter_context(tc.tile_pool(name="const", bufs=1))
         x_pool = ctx.enter_context(tc.tile_pool(name="x_pool", bufs=6))
-        band_pool = ctx.enter_context(tc.tile_pool(name="band_pool", bufs=3))
+        band_pool = ctx.enter_context(tc.tile_pool(name="band_pool", bufs=4))
         haar_pool = ctx.enter_context(tc.tile_pool(name="haar_pool", bufs=2))
         stat_pool = ctx.enter_context(tc.tile_pool(name="stat_pool", bufs=2))
         u_pool = ctx.enter_context(tc.tile_pool(name="u_pool", bufs=2))
@@ -47,7 +49,6 @@ def tile_shiftedpatchtokenization_pb_t_kernel(tc, x, ln2_g, ln2_b, w2_words, w2_
         psum_stat = ctx.enter_context(tc.psum_pool(name="psum_stat", bufs=1))
 
         x_body = x.rearrange("b c (q r) w -> b (c q) (r w)", q=4)
-        x_plane = x.rearrange("b (l c) h w -> l b c (h w)", c=2)
         tok_rows = tok.rearrange("b t n -> (b t) n").rearrange("(m s) n -> m s n", s=64)
         out_rows = out.rearrange("b t n -> (b t) n").rearrange("(m s) n -> m s n", s=64)
 
@@ -74,7 +75,7 @@ def tile_shiftedpatchtokenization_pb_t_kernel(tc, x, ln2_g, ln2_b, w2_words, w2_
         nc.vector.tensor_copy(out=gain[:], in_=gain_bf[:])
         nc.vector.tensor_copy(out=bias[:], in_=bias_bf[:])
 
-        quad_sums = const.tile([P, 2, 2 * BANDS, 34], F32)
+        quad_sums = const.tile([P, 2, 2 * BANDS, QUAD_PITCH], F32)
         nc.vector.memset(quad_sums[:], 0.0)
 
         w_codes = const.tile([P, PASSES, DIM], U32, align_bytes=64)
@@ -94,74 +95,85 @@ def tile_shiftedpatchtokenization_pb_t_kernel(tc, x, ln2_g, ln2_b, w2_words, w2_
             )
             nc.sync.dma_start(out=b2_all[:], in_=b2.partition_broadcast(P))
 
-        bands = []
+        bands = {}
 
-        def haar_band(kb):
+        def new_band(kb):
             band = band_pool.tile([P, PLANES, BAND_ROWS, PADDED], F32, name="band")
-            bands.append(band)
+            bands[kb] = band
             nc.vector.memset(band[:, :, :, 0:4], 0.0)
             nc.vector.memset(band[:, :, :, PADDED - 4 : PADDED], 0.0)
-            for l in range(PLANES):
-                xt = x_pool.tile([P, 2 * BAND_ROWS, 256], BF16, name="xt")
-                first = 16 * kb - 8
-                lo = max(first, 0)
-                hi = min(first + 16, 64)
-                if kb == 0:
-                    nc.vector.memset(xt[:, 0:8, :], 0.0)
-                    for q in range(1, 4):
-                        nc.sync.dma_start(
-                            out=xt[q:P:4, 0:8, :].rearrange("p r w -> p (r w)"),
-                            in_=x_plane[l][:, :, (64 * q - 8) * 256 : 64 * q * 256],
-                        )
-                if kb == BANDS - 1:
-                    nc.vector.memset(xt[:, 8:16, :], 0.0)
-                    for q in range(0, 3):
-                        nc.sync.dma_start(
-                            out=xt[q:P:4, 8:16, :].rearrange("p r w -> p (r w)"),
-                            in_=x_plane[l][:, :, (64 * q + 64) * 256 : (64 * q + 72) * 256],
-                        )
+            return band
+
+        def haar_rows(l, loads, stores):
+            xt = x_pool.tile([P, 2 * BAND_ROWS, 256], BF16, name="xt")
+            for at, first, count in loads:
                 nc.sync.dma_start(
-                    out=xt[:, lo - first : hi - first, :].rearrange("p r w -> p (r w)"),
-                    in_=x_body[:, 8 * l : 8 * l + 8, lo * 256 : hi * 256],
+                    out=xt[:, at : at + count, :].rearrange("p r w -> p (r w)"),
+                    in_=x_body[:, 8 * l : 8 * l + 8, first * 256 : (first + count) * 256],
                 )
-                blocks = xt[:].rearrange("p (r v) (w h) -> p r v w h", v=2, h=2)
-                rest = haar_pool.tile([P, BAND_ROWS, 128], F32, name="rest")
-                nc.vector.tensor_tensor(out=rest[:], in0=blocks[:, :, 1, :, 0], in1=blocks[:, :, 1, :, 1], op=ALU.add)
-                nc.vector.tensor_tensor(out=rest[:], in0=rest[:], in1=blocks[:, :, 0, :, 1], op=ALU.add)
+            blocks = xt[:].rearrange("p (r v) (w h) -> p r v w h", v=2, h=2)
+            rest = haar_pool.tile([P, BAND_ROWS, 128], F32, name="rest")
+            nc.vector.tensor_tensor(out=rest[:], in0=blocks[:, :, 1, :, 0], in1=blocks[:, :, 1, :, 1], op=ALU.add)
+            nc.vector.tensor_tensor(out=rest[:], in0=rest[:], in1=blocks[:, :, 0, :, 1], op=ALU.add)
+            for band, to_row, from_row, count in stores:
                 nc.vector.scalar_tensor_tensor(
-                    out=band[:, l, :, 4 : PADDED - 4],
-                    in0=blocks[:, :, 0, :, 0],
+                    out=band[:, l, to_row : to_row + count, 4 : PADDED - 4],
+                    in0=blocks[:, from_row : from_row + count, 0, :, 0],
                     scalar=3.0,
-                    in1=rest[:],
+                    in1=rest[:, from_row : from_row + count, :],
                     op0=ALU.mult,
                     op1=ALU.subtract,
                 )
-            bn = stat_pool.tile([P, 2, 32, 6], F32, name="bn")
-            for yq in range(2):
-                for xq in range(32):
+
+        def square_sums(halves, rows):
+            bn = stat_pool.tile([P, 2, 16, 6], F32, name="bn")
+            for yq, (band, row) in enumerate(halves):
+                for xp in range(16):
                     nc.vector.bn_stats(
-                        out=bn[:, yq, xq, :],
-                        in_=band[:, :, 4 * yq : 4 * yq + 4, 4 + 4 * xq : 8 + 4 * xq],
+                        out=bn[:, yq, xp, :],
+                        in_=band[:, :, row : row + 4, 4 + 8 * xp : 12 + 8 * xp].rearrange(
+                            "p l r (c s) -> p l r s c", c=2
+                        ),
                     )
-            squares = stat_pool.tile([P, 2, 32, 2], F32, name="squares")
+            squares = stat_pool.tile([P, 2, 16, 2], F32, name="squares")
             nc.vector.tensor_tensor(out=squares[:], in0=bn[:, :, :, 1:6:3], in1=bn[:, :, :, 1:6:3], op=ALU.mult)
+            nc.vector.tensor_copy(
+                out=quad_sums[:, 0, rows, 1:33].rearrange("p y (x c) -> p y x c", c=2), in_=bn[:, :, :, 1:6:3]
+            )
             nc.vector.scalar_tensor_tensor(
-                out=squares[:], in0=squares[:], scalar=32.0, in1=bn[:, :, :, 2:6:3], op0=ALU.mult, op1=ALU.add
+                out=quad_sums[:, 1, rows, 1:33].rearrange("p y (x c) -> p y x c", c=2),
+                in0=squares[:], scalar=64.0, in1=bn[:, :, :, 2:6:3], op0=ALU.mult, op1=ALU.add,
             )
-            rows = slice(2 * kb, 2 * kb + 2)
-            nc.vector.tensor_tensor(out=quad_sums[:, 0, rows, 1:33], in0=bn[:, :, :, 1], in1=bn[:, :, :, 4], op=ALU.add)
-            nc.vector.tensor_tensor(
-                out=quad_sums[:, 1, rows, 1:33], in0=squares[:, :, :, 0], in1=squares[:, :, :, 1], op=ALU.add
-            )
+
+        def haar_band(kb):
+            band = new_band(kb)
+            for l in range(PLANES):
+                haar_rows(l, ((0, 16 * kb - 8, 16),), ((band, 0, 0, BAND_ROWS),))
+            square_sums(((band, 0), (band, 4)), slice(2 * kb, 2 * kb + 2))
+
+        def haar_edges():
+            top = new_band(0)
+            bottom = new_band(BANDS - 1)
+            nc.gpsimd.memset(top[:, :, 0:4, :], 0.0)
+            nc.gpsimd.memset(bottom[:, :, 4:8, :], 0.0)
+            for l in range(PLANES):
+                haar_rows(l, ((0, 0, 8), (8, 56, 8)), ((top, 4, 0, 4), (bottom, 0, 4, 4)))
+            square_sums(((top, 4), (bottom, 0)), slice(1, 9, 7))
+            for q in range(1, 4):
+                nc.sync.dma_start(out=top[q:P:4, :, 0:4, :], in_=bottom[q - 1 : P : 4, :, 0:4, :])
+                nc.sync.dma_start(out=quad_sums[q:P:4, :, 0, :], in_=quad_sums[q - 1 : P : 4, :, 8, :])
+            for q in range(1, 4):
+                nc.sync.dma_start(out=bottom[q - 1 : P : 4, :, 4:8, :], in_=top[q:P:4, :, 4:8, :])
+                nc.sync.dma_start(out=quad_sums[q - 1 : P : 4, :, 9, :], in_=quad_sums[q:P:4, :, 1, :])
 
         def token_stats(i):
             inner = stat_pool.tile([P, 2, 34], F32, name="inner")
             outer = stat_pool.tile([P, 2, 34], F32, name="outer")
             nc.vector.tensor_tensor(
-                out=inner[:], in0=quad_sums[:, :, 2 * i + 1, :], in1=quad_sums[:, :, 2 * i + 2, :], op=ALU.add
+                out=inner[:], in0=quad_sums[:, :, 2 * i + 1, 0:34], in1=quad_sums[:, :, 2 * i + 2, 0:34], op=ALU.add
             )
             nc.vector.tensor_tensor(
-                out=outer[:], in0=quad_sums[:, :, 2 * i, :], in1=quad_sums[:, :, 2 * i + 3, :], op=ALU.add
+                out=outer[:], in0=quad_sums[:, :, 2 * i, 0:34], in1=quad_sums[:, :, 2 * i + 3, 0:34], op=ALU.add
             )
             nc.vector.tensor_tensor(out=outer[:], in0=outer[:], in1=inner[:], op=ALU.add)
             nc.vector.tensor_tensor(out=inner[:], in0=inner[:], in1=outer[:], op=ALU.add)
@@ -178,7 +190,7 @@ def tile_shiftedpatchtokenization_pb_t_kernel(tc, x, ln2_g, ln2_b, w2_words, w2_
             std = stat_pool.tile([P, 16], F32, name="std")
             rstd = stat_pool.tile([P, 16], F32, name="rstd")
             shift = stat_pool.tile([P, 16], F32, name="shift")
-            nc.vector.tensor_scalar(out=mean[:], in0=both[:, 0:16], scalar1=32.0 / K, scalar2=None, op0=ALU.mult)
+            nc.vector.tensor_scalar(out=mean[:], in0=both[:, 0:16], scalar1=64.0 / K, scalar2=None, op0=ALU.mult)
             nc.vector.tensor_scalar(
                 out=var[:], in0=both[:, 16:32], scalar1=1.0 / K, scalar2=36.0 * EPS, op0=ALU.mult, op1=ALU.add
             )
@@ -218,7 +230,7 @@ def tile_shiftedpatchtokenization_pb_t_kernel(tc, x, ln2_g, ln2_b, w2_words, w2_
             u = u_pool.tile([P, GROUP, WORDS], F32, name="u")
             for jl in range(GROUP):
                 j = GROUP * jc + jl
-                on_vector = jl == GROUP - 1
+                on_vector = jl >= GROUP - VECTOR_PATCHES[i]
                 uv = u[:, jl, :].rearrange("p (a b c l) -> p a b c l", a=8, b=8, c=5, l=PLANES)
                 x0 = 8 * j
                 normalise(
@@ -280,12 +292,12 @@ def tile_shiftedpatchtokenization_pb_t_kernel(tc, x, ln2_g, ln2_b, w2_words, w2_
                 nc.vector.tensor_tensor(out=result[:], in0=acc[:], in1=tok_tiles[jp][:], op=ALU.add)
                 nc.sync.dma_start(out=out_rows[:, s0 : s0 + 2, :], in_=result[:])
 
-        haar_band(0)
+        haar_edges()
         haar_band(1)
         load_weights()
         for i in range(TOKEN_ROWS):
             stats = token_stats(i)
-            if i + 2 < BANDS:
+            if i + 2 < BANDS - 1:
                 haar_band(i + 2)
             for jc in range(GROUPS):
                 patch_group(i, jc, stats)

@@ -43,10 +43,10 @@ def tile_shiftedpatchtokenization_pb_t_kernel(tc, x, ln2_g, ln2_b, w2_words, w2_
         u_pool = ctx.enter_context(tc.tile_pool(name="u_pool", bufs=2))
         z_pool = ctx.enter_context(tc.tile_pool(name="z_pool", bufs=3))
         code_pool = ctx.enter_context(tc.tile_pool(name="code_pool", bufs=2))
-        io_pool = ctx.enter_context(tc.tile_pool(name="io_pool", bufs=4))
+        io_pool = ctx.enter_context(tc.tile_pool(name="io_pool", bufs=3))
+        tok_pool = ctx.enter_context(tc.tile_pool(name="tok_pool", bufs=6))
         psum_t = ctx.enter_context(tc.psum_pool(name="psum_t", bufs=4))
-        psum_mx = ctx.enter_context(tc.psum_pool(name="psum_mx", bufs=2))
-        psum_stat = ctx.enter_context(tc.psum_pool(name="psum_stat", bufs=1))
+        psum_mx = ctx.enter_context(tc.psum_pool(name="psum_mx", bufs=4))
 
         x_body = x.rearrange("b c (q r) w -> b (c q) (r w)", q=4)
         tok_rows = tok.rearrange("b t n -> (b t) n").rearrange("(m s) n -> m s n", s=64)
@@ -182,7 +182,7 @@ def tile_shiftedpatchtokenization_pb_t_kernel(tc, x, ln2_g, ln2_b, w2_words, w2_
             nc.vector.tensor_tensor(out=sums[:], in0=inner[:, :, 1:33:2], in1=inner[:, :, 2:34:2], op=ALU.add)
             nc.vector.tensor_tensor(out=edge[:], in0=outer[:, :, 0:32:2], in1=outer[:, :, 3:34:2], op=ALU.add)
             nc.vector.tensor_tensor(out=sums[:], in0=sums[:], in1=edge[:], op=ALU.add)
-            both = psum_stat.tile([P, 32], F32, name="both")
+            both = psum_t.tile([P, 32], F32, name="turned")
             nc.tensor.matmul(out=both[:], lhsT=pair[:], rhs=sums[:].rearrange("p s j -> p (s j)"), start=True, stop=True)
             mean = stat_pool.tile([P, 16], F32, name="mean")
             var = stat_pool.tile([P, 16], F32, name="var")
@@ -215,7 +215,31 @@ def tile_shiftedpatchtokenization_pb_t_kernel(tc, x, ln2_g, ln2_b, w2_words, w2_
                     out=dst, in_=src, func=ACT.Identity, bias=shift[:, j : j + 1], scale=rstd[:, j : j + 1]
                 )
 
-        def patch_group(i, jc, stats):
+        def multiply(group, g):
+            if g == 0:
+                for jp in range(2):
+                    acc = psum_mx.tile([P, DIM], F32, name="acc")
+                    group["acc"].append(acc)
+            for jp in range(2):
+                cols = slice(P * jp, P * jp + P)
+                nc.tensor.matmul_mx(
+                    out=group["acc"][jp][:],
+                    lhsT=group["codes"][:, g, cols].bitcast(FP8X4),
+                    lhsT_scale=group["scales"][:, g, cols],
+                    rhs=w_codes[:, g, :].bitcast(FP8X4),
+                    rhs_scale=w_scales[:, g, :],
+                    start=(g == 0),
+                    stop=(g == PASSES - 1),
+                )
+
+        def finish(group):
+            for jp in range(2):
+                s0 = group["s0"] + 2 * jp
+                result = io_pool.tile([P, DIM], F32, name="result")
+                nc.vector.tensor_tensor(out=result[:], in0=group["acc"][jp][:], in1=group["tok"][jp][:], op=ALU.add)
+                nc.sync.dma_start(out=out_rows[:, s0 : s0 + 2, :], in_=result[:])
+
+        def patch_group(i, jc, stats, before):
             upper = bands[i]
             lower = bands[i + 1]
             tok_tiles = []
@@ -223,7 +247,7 @@ def tile_shiftedpatchtokenization_pb_t_kernel(tc, x, ln2_g, ln2_b, w2_words, w2_
                 s0 = 16 * i + GROUP * jc + 2 * jp
                 tok_bf = io_pool.tile([P, DIM], BF16, name="tok_bf")
                 nc.sync.dma_start(out=tok_bf[:], in_=tok_rows[:, s0 : s0 + 2, :])
-                tok_b2 = io_pool.tile([P, DIM], F32, name="tok_b2")
+                tok_b2 = tok_pool.tile([P, DIM], F32, name="tok_b2")
                 nc.gpsimd.tensor_tensor(out=tok_b2[:], in0=tok_bf[:], in1=b2_all[:], op=ALU.add)
                 tok_tiles.append(tok_b2)
 
@@ -273,31 +297,26 @@ def tile_shiftedpatchtokenization_pb_t_kernel(tc, x, ln2_g, ln2_b, w2_words, w2_
                     out=grouped[:].rearrange("p (w t) -> p w t", t=4), in_=planes[:].rearrange("p t w -> p w t")
                 )
                 nc.vector.quantize_mx(out=z_codes[:, g, :].bitcast(FP8X4), scales=z_scales[:, g, :], in_=grouped[:])
+                if before is not None:
+                    multiply(before, g)
 
-            for jp in range(2):
-                s0 = 16 * i + GROUP * jc + 2 * jp
-                cols = slice(P * jp, P * jp + P)
-                acc = psum_mx.tile([P, DIM], F32, name="acc")
-                for g in range(PASSES):
-                    nc.tensor.matmul_mx(
-                        out=acc[:],
-                        lhsT=z_codes[:, g, cols].bitcast(FP8X4),
-                        lhsT_scale=z_scales[:, g, cols],
-                        rhs=w_codes[:, g, :].bitcast(FP8X4),
-                        rhs_scale=w_scales[:, g, :],
-                        start=(g == 0),
-                        stop=(g == PASSES - 1),
-                    )
-                result = io_pool.tile([P, DIM], F32, name="result")
-                nc.vector.tensor_tensor(out=result[:], in0=acc[:], in1=tok_tiles[jp][:], op=ALU.add)
-                nc.sync.dma_start(out=out_rows[:, s0 : s0 + 2, :], in_=result[:])
+            if before is not None:
+                finish(before)
+            return {"codes": z_codes, "scales": z_scales, "tok": tok_tiles, "s0": 16 * i + GROUP * jc, "acc": []}
 
-        haar_edges()
-        haar_band(1)
-        load_weights()
-        for i in range(TOKEN_ROWS):
-            stats = token_stats(i)
-            if i + 2 < BANDS - 1:
-                haar_band(i + 2)
-            for jc in range(GROUPS):
-                patch_group(i, jc, stats)
+        with tc.manual_schedule(engines={mybir.EngineType.PE}):
+            haar_edges()
+            haar_band(1)
+            load_weights()
+            stats = {0: token_stats(0)}
+            before = None
+            for i in range(TOKEN_ROWS):
+                if i + 2 < BANDS - 1:
+                    haar_band(i + 2)
+                for jc in range(GROUPS):
+                    if jc == GROUPS - 1 and i + 1 < TOKEN_ROWS:
+                        stats[i + 1] = token_stats(i + 1)
+                    before = patch_group(i, jc, stats[i], before)
+            for g in range(PASSES):
+                multiply(before, g)
+            finish(before)

@@ -66,6 +66,11 @@ def tile_shiftedpatchtokenization_pb_t_kernel(tc, x, ln2_g, ln2_b, w2_words, w2_
         nc.vector.tensor_copy(out=pair_bcq[:, :, 1, :], in_=ident_bcq[:, :, 0, :])
         nc.vector.tensor_tensor(out=pair[:], in0=pair[:], in1=ident[:], op=ALU.add)
 
+        three_eye = const.tile([P, P], BF16)
+        minus_eye = const.tile([P, P], BF16)
+        nc.vector.tensor_scalar(out=three_eye[:], in0=ident[:], scalar1=3.0, scalar2=None, op0=ALU.mult)
+        nc.vector.tensor_scalar(out=minus_eye[:], in0=ident[:], scalar1=-1.0, scalar2=None, op0=ALU.mult)
+
         gain_bf = const.tile([P, PASSES, 4], BF16)
         bias_bf = const.tile([P, PASSES, 4], BF16)
         nc.sync.dma_start(out=gain_bf[:], in_=ln2_g.rearrange("(g p t) -> p g t", g=PASSES, p=P, t=4))
@@ -104,26 +109,40 @@ def tile_shiftedpatchtokenization_pb_t_kernel(tc, x, ln2_g, ln2_b, w2_words, w2_
             nc.vector.memset(band[:, :, :, PADDED - 4 : PADDED], 0.0)
             return band
 
-        def haar_rows(l, loads, stores):
+        def load_x(l, loads):
             xt = x_pool.tile([P, 2 * BAND_ROWS, 256], BF16, name="xt")
             for at, first, count in loads:
                 nc.sync.dma_start(
                     out=xt[:, at : at + count, :].rearrange("p r w -> p (r w)"),
                     in_=x_body[:, 8 * l : 8 * l + 8, first * 256 : (first + count) * 256],
                 )
-            blocks = xt[:].rearrange("p (r v) (w h) -> p r v w h", v=2, h=2)
+            return xt[:].rearrange("p (r v) (w h) -> p r v w h", v=2, h=2)
+
+        def detail_on_vector(blocks, r0, count, dest):
+            rows = slice(r0, r0 + count)
             rest = haar_pool.tile([P, BAND_ROWS, 128], F32, name="rest")
-            nc.vector.tensor_tensor(out=rest[:], in0=blocks[:, :, 1, :, 0], in1=blocks[:, :, 1, :, 1], op=ALU.add)
-            nc.vector.tensor_tensor(out=rest[:], in0=rest[:], in1=blocks[:, :, 0, :, 1], op=ALU.add)
-            for band, to_row, from_row, count in stores:
-                nc.vector.scalar_tensor_tensor(
-                    out=band[:, l, to_row : to_row + count, 4 : PADDED - 4],
-                    in0=blocks[:, from_row : from_row + count, 0, :, 0],
-                    scalar=3.0,
-                    in1=rest[:, from_row : from_row + count, :],
-                    op0=ALU.mult,
-                    op1=ALU.subtract,
+            nc.vector.tensor_tensor(
+                out=rest[:, 0:count, :], in0=blocks[:, rows, 1, :, 0], in1=blocks[:, rows, 1, :, 1], op=ALU.add
+            )
+            nc.vector.tensor_tensor(
+                out=rest[:, 0:count, :], in0=rest[:, 0:count, :], in1=blocks[:, rows, 0, :, 1], op=ALU.add
+            )
+            nc.vector.scalar_tensor_tensor(
+                out=dest, in0=blocks[:, rows, 0, :, 0], scalar=3.0, in1=rest[:, 0:count, :],
+                op0=ALU.mult, op1=ALU.subtract,
+            )
+
+        def detail_on_tensor(blocks, r0, dest):
+            detail = psum_t.tile([P, 4, P], F32, name="turned")
+            for step, (v, h) in enumerate(((0, 0), (0, 1), (1, 0), (1, 1))):
+                nc.tensor.matmul(
+                    out=detail[:],
+                    lhsT=(three_eye if step == 0 else minus_eye)[:],
+                    rhs=blocks[:, r0 : r0 + 4, v, :, h],
+                    start=(step == 0),
+                    stop=(step == 3),
                 )
+            nc.scalar.copy(out=dest, in_=detail[:])
 
         def square_sums(halves, rows):
             bn = stat_pool.tile([P, 2, 16, 6], F32, name="bn")
@@ -145,10 +164,15 @@ def tile_shiftedpatchtokenization_pb_t_kernel(tc, x, ln2_g, ln2_b, w2_words, w2_
                 in0=squares[:], scalar=64.0, in1=bn[:, :, :, 2:6:3], op0=ALU.mult, op1=ALU.add,
             )
 
-        def haar_band(kb):
+        def haar_band(kb, on_tensor):
             band = new_band(kb)
             for l in range(PLANES):
-                haar_rows(l, ((0, 16 * kb - 8, 16),), ((band, 0, 0, BAND_ROWS),))
+                blocks = load_x(l, ((0, 16 * kb - 8, 16),))
+                if on_tensor:
+                    detail_on_tensor(blocks, 0, band[:, l, 0:4, 4 : PADDED - 4])
+                    detail_on_tensor(blocks, 4, band[:, l, 4:8, 4 : PADDED - 4])
+                else:
+                    detail_on_vector(blocks, 0, BAND_ROWS, band[:, l, :, 4 : PADDED - 4])
             square_sums(((band, 0), (band, 4)), slice(2 * kb, 2 * kb + 2))
 
         def haar_edges():
@@ -157,7 +181,12 @@ def tile_shiftedpatchtokenization_pb_t_kernel(tc, x, ln2_g, ln2_b, w2_words, w2_
             nc.gpsimd.memset(top[:, :, 0:4, :], 0.0)
             nc.gpsimd.memset(bottom[:, :, 4:8, :], 0.0)
             for l in range(PLANES):
-                haar_rows(l, ((0, 0, 8), (8, 56, 8)), ((top, 4, 0, 4), (bottom, 0, 4, 4)))
+                blocks = load_x(l, ((0, 0, 8), (8, 56, 8)))
+                detail_on_tensor(blocks, 0, top[:, l, 4:8, 4 : PADDED - 4])
+                if l < PLANES - 1:
+                    detail_on_tensor(blocks, 4, bottom[:, l, 0:4, 4 : PADDED - 4])
+                else:
+                    detail_on_vector(blocks, 4, 4, bottom[:, l, 0:4, 4 : PADDED - 4])
             square_sums(((top, 4), (bottom, 0)), slice(1, 9, 7))
             for q in range(1, 4):
                 nc.sync.dma_start(out=top[q:P:4, :, 0:4, :], in_=bottom[q - 1 : P : 4, :, 0:4, :])
@@ -306,13 +335,13 @@ def tile_shiftedpatchtokenization_pb_t_kernel(tc, x, ln2_g, ln2_b, w2_words, w2_
 
         with tc.manual_schedule(engines={mybir.EngineType.PE}):
             haar_edges()
-            haar_band(1)
+            haar_band(1, True)
             load_weights()
             stats = {0: token_stats(0)}
             before = None
             for i in range(TOKEN_ROWS):
                 if i + 2 < BANDS - 1:
-                    haar_band(i + 2)
+                    haar_band(i + 2, False)
                 for jc in range(GROUPS):
                     if jc == GROUPS - 1 and i + 1 < TOKEN_ROWS:
                         stats[i + 1] = token_stats(i + 1)

@@ -28,6 +28,7 @@ GROUP = 4
 GROUPS = 16 // GROUP
 WORDS = K // 2
 VECTOR_PATCHES = (1, 1, 3, 3)
+MULTIPLY_BEHIND = (1, 4)
 
 FLOPS = 2 * BATCH * 256 * K * DIM
 
@@ -45,8 +46,8 @@ def tile_shiftedpatchtokenization_pb_t_kernel(tc, x, ln2_g, ln2_b, w2_words, w2_
         code_pool = ctx.enter_context(tc.tile_pool(name="code_pool", bufs=2))
         io_pool = ctx.enter_context(tc.tile_pool(name="io_pool", bufs=3))
         tok_pool = ctx.enter_context(tc.tile_pool(name="tok_pool", bufs=6))
-        psum_t = ctx.enter_context(tc.psum_pool(name="psum_t", bufs=4))
-        psum_mx = ctx.enter_context(tc.psum_pool(name="psum_mx", bufs=4))
+        psum_t = ctx.enter_context(tc.psum_pool(name="psum_t", bufs=5))
+        psum_mx = ctx.enter_context(tc.psum_pool(name="psum_mx", bufs=3))
 
         x_body = x.rearrange("b c (q r) w -> b (c q) (r w)", q=4)
         tok_rows = tok.rearrange("b t n -> (b t) n").rearrange("(m s) n -> m s n", s=64)
@@ -244,15 +245,12 @@ def tile_shiftedpatchtokenization_pb_t_kernel(tc, x, ln2_g, ln2_b, w2_words, w2_
                     out=dst, in_=src, func=ACT.Identity, bias=shift[:, j : j + 1], scale=rstd[:, j : j + 1]
                 )
 
-        def multiply(group, g):
-            if g == 0:
-                for jp in range(2):
-                    acc = psum_mx.tile([P, DIM], F32, name="acc")
-                    group["acc"].append(acc)
-            for jp in range(2):
-                cols = slice(P * jp, P * jp + P)
+        def multiply(group, jp):
+            cols = slice(P * jp, P * jp + P)
+            acc = psum_mx.tile([P, DIM], F32, name="acc")
+            for g in range(PASSES):
                 nc.tensor.matmul_mx(
-                    out=group["acc"][jp][:],
+                    out=acc[:],
                     lhsT=group["codes"][:, g, cols].bitcast(FP8X4),
                     lhsT_scale=group["scales"][:, g, cols],
                     rhs=w_codes[:, g, :].bitcast(FP8X4),
@@ -260,13 +258,10 @@ def tile_shiftedpatchtokenization_pb_t_kernel(tc, x, ln2_g, ln2_b, w2_words, w2_
                     start=(g == 0),
                     stop=(g == PASSES - 1),
                 )
-
-        def finish(group):
-            for jp in range(2):
-                s0 = group["s0"] + 2 * jp
-                result = io_pool.tile([P, DIM], F32, name="result")
-                nc.vector.tensor_tensor(out=result[:], in0=group["acc"][jp][:], in1=group["tok"][jp][:], op=ALU.add)
-                nc.sync.dma_start(out=out_rows[:, s0 : s0 + 2, :], in_=result[:])
+            s0 = group["s0"] + 2 * jp
+            result = io_pool.tile([P, DIM], F32, name="result")
+            nc.vector.tensor_tensor(out=result[:], in0=acc[:], in1=group["tok"][jp][:], op=ALU.add)
+            nc.sync.dma_start(out=out_rows[:, s0 : s0 + 2, :], in_=result[:])
 
         def patch_group(i, jc, stats, before):
             upper = bands[i]
@@ -326,12 +321,10 @@ def tile_shiftedpatchtokenization_pb_t_kernel(tc, x, ln2_g, ln2_b, w2_words, w2_
                     out=grouped[:].rearrange("p (w t) -> p w t", t=4), in_=planes[:].rearrange("p t w -> p w t")
                 )
                 nc.vector.quantize_mx(out=z_codes[:, g, :].bitcast(FP8X4), scales=z_scales[:, g, :], in_=grouped[:])
-                if before is not None:
-                    multiply(before, g)
+                if before is not None and g in MULTIPLY_BEHIND:
+                    multiply(before, MULTIPLY_BEHIND.index(g))
 
-            if before is not None:
-                finish(before)
-            return {"codes": z_codes, "scales": z_scales, "tok": tok_tiles, "s0": 16 * i + GROUP * jc, "acc": []}
+            return {"codes": z_codes, "scales": z_scales, "tok": tok_tiles, "s0": 16 * i + GROUP * jc}
 
         with tc.manual_schedule(engines={mybir.EngineType.PE}):
             haar_edges()
@@ -346,6 +339,5 @@ def tile_shiftedpatchtokenization_pb_t_kernel(tc, x, ln2_g, ln2_b, w2_words, w2_
                     if jc == GROUPS - 1 and i + 1 < TOKEN_ROWS:
                         stats[i + 1] = token_stats(i + 1)
                     before = patch_group(i, jc, stats[i], before)
-            for g in range(PASSES):
-                multiply(before, g)
-            finish(before)
+            for jp in range(2):
+                multiply(before, jp)

@@ -318,7 +318,8 @@ def tile_shiftedpatchtokenization_pb_t_kernel(tc, x, ln2_g, ln2_b, w2_words, w2_
                         )
                 grouped = z_pool.tile([P, 4 * GROUP * 64], BF16, name="grouped", align_bytes=64)
                 nc.vector.tensor_copy(
-                    out=grouped[:].rearrange("p (w t) -> p w t", t=4), in_=planes[:].rearrange("p t w -> p w t")
+                    out=grouped[:].rearrange("p (c i t) -> p c t i", i=4, t=4),
+                    in_=planes[:].rearrange("p t (c i) -> p c t i", i=4),
                 )
                 nc.vector.quantize_mx(out=z_codes[:, g, :].bitcast(FP8X4), scales=z_scales[:, g, :], in_=grouped[:])
                 if before is not None and g in MULTIPLY_BEHIND:

@@ -28,6 +28,7 @@ GROUP = 4
 GROUPS = 16 // GROUP
 WORDS = K // 2
 VECTOR_PATCHES = (1, 1, 3, 3)
+HEAD_TENSOR_PLANES = (1, 3)
 MULTIPLY_BEHIND = (1, 4)
 
 FLOPS = 2 * BATCH * 256 * K * DIM
@@ -119,19 +120,15 @@ def tile_shiftedpatchtokenization_pb_t_kernel(tc, x, ln2_g, ln2_b, w2_words, w2_
                 )
             return xt[:].rearrange("p (r v) (w h) -> p r v w h", v=2, h=2)
 
-        def detail_on_vector(blocks, r0, count, dest):
-            rows = slice(r0, r0 + count)
+        def detail_on_vector(blocks, dests):
             rest = haar_pool.tile([P, BAND_ROWS, 128], F32, name="rest")
-            nc.vector.tensor_tensor(
-                out=rest[:, 0:count, :], in0=blocks[:, rows, 1, :, 0], in1=blocks[:, rows, 1, :, 1], op=ALU.add
-            )
-            nc.vector.tensor_tensor(
-                out=rest[:, 0:count, :], in0=rest[:, 0:count, :], in1=blocks[:, rows, 0, :, 1], op=ALU.add
-            )
-            nc.vector.scalar_tensor_tensor(
-                out=dest, in0=blocks[:, rows, 0, :, 0], scalar=3.0, in1=rest[:, 0:count, :],
-                op0=ALU.mult, op1=ALU.subtract,
-            )
+            nc.vector.tensor_tensor(out=rest[:], in0=blocks[:, :, 1, :, 0], in1=blocks[:, :, 1, :, 1], op=ALU.add)
+            nc.vector.tensor_tensor(out=rest[:], in0=rest[:], in1=blocks[:, :, 0, :, 1], op=ALU.add)
+            for dest, r0, count in dests:
+                nc.vector.scalar_tensor_tensor(
+                    out=dest, in0=blocks[:, r0 : r0 + count, 0, :, 0], scalar=3.0, in1=rest[:, r0 : r0 + count, :],
+                    op0=ALU.mult, op1=ALU.subtract,
+                )
 
         def detail_on_tensor(blocks, r0, dest):
             detail = psum_t.tile([P, 4, P], F32, name="turned")
@@ -165,29 +162,31 @@ def tile_shiftedpatchtokenization_pb_t_kernel(tc, x, ln2_g, ln2_b, w2_words, w2_
                 in0=squares[:], scalar=64.0, in1=bn[:, :, :, 2:6:3], op0=ALU.mult, op1=ALU.add,
             )
 
-        def haar_band(kb, on_tensor):
+        def haar_band(kb, tensor_planes):
             band = new_band(kb)
             for l in range(PLANES):
                 blocks = load_x(l, ((0, 16 * kb - 8, 16),))
-                if on_tensor:
+                if l in tensor_planes:
                     detail_on_tensor(blocks, 0, band[:, l, 0:4, 4 : PADDED - 4])
                     detail_on_tensor(blocks, 4, band[:, l, 4:8, 4 : PADDED - 4])
                 else:
-                    detail_on_vector(blocks, 0, BAND_ROWS, band[:, l, :, 4 : PADDED - 4])
+                    detail_on_vector(blocks, ((band[:, l, :, 4 : PADDED - 4], 0, BAND_ROWS),))
             square_sums(((band, 0), (band, 4)), slice(2 * kb, 2 * kb + 2))
 
-        def haar_edges():
+        def haar_edges(tensor_planes):
             top = new_band(0)
             bottom = new_band(BANDS - 1)
             nc.gpsimd.memset(top[:, :, 0:4, :], 0.0)
             nc.gpsimd.memset(bottom[:, :, 4:8, :], 0.0)
             for l in range(PLANES):
                 blocks = load_x(l, ((0, 0, 8), (8, 56, 8)))
-                detail_on_tensor(blocks, 0, top[:, l, 4:8, 4 : PADDED - 4])
-                if l < PLANES - 1:
+                if l in tensor_planes:
+                    detail_on_tensor(blocks, 0, top[:, l, 4:8, 4 : PADDED - 4])
                     detail_on_tensor(blocks, 4, bottom[:, l, 0:4, 4 : PADDED - 4])
                 else:
-                    detail_on_vector(blocks, 4, 4, bottom[:, l, 0:4, 4 : PADDED - 4])
+                    detail_on_vector(
+                        blocks, ((top[:, l, 4:8, 4 : PADDED - 4], 0, 4), (bottom[:, l, 0:4, 4 : PADDED - 4], 4, 4))
+                    )
             square_sums(((top, 4), (bottom, 0)), slice(1, 9, 7))
             for q in range(1, 4):
                 nc.sync.dma_start(out=top[q:P:4, :, 0:4, :], in_=bottom[q - 1 : P : 4, :, 0:4, :])
@@ -328,14 +327,14 @@ def tile_shiftedpatchtokenization_pb_t_kernel(tc, x, ln2_g, ln2_b, w2_words, w2_
             return {"codes": z_codes, "scales": z_scales, "tok": tok_tiles, "s0": 16 * i + GROUP * jc}
 
         with tc.manual_schedule(engines={mybir.EngineType.PE}):
-            haar_edges()
-            haar_band(1, True)
+            haar_edges(HEAD_TENSOR_PLANES)
+            haar_band(1, HEAD_TENSOR_PLANES)
             load_weights()
             stats = {0: token_stats(0)}
             before = None
             for i in range(TOKEN_ROWS):
                 if i + 2 < BANDS - 1:
-                    haar_band(i + 2, False)
+                    haar_band(i + 2, ())
                 for jc in range(GROUPS):
                     if jc == GROUPS - 1 and i + 1 < TOKEN_ROWS:
                         stats[i + 1] = token_stats(i + 1)

@@ -28,8 +28,12 @@ GROUP = 4
 GROUPS = 16 // GROUP
 WORDS = K // 2
 VECTOR_PATCHES = (1, 1, 3, 3)
+FIRST_VECTOR_PATCHES = 3
 HEAD_TENSOR_PLANES = (1, 3)
-MULTIPLY_BEHIND = (1, 4)
+LATER_TENSOR_PLANES = ((1, 3), (1,))
+STATS_AT = (2, 3)
+COPY_UNITS = ((0, 1), (2, 3), (4,))
+MULTIPLY_BEHIND = (2, 4)
 
 FLOPS = 2 * BATCH * 256 * K * DIM
 
@@ -43,7 +47,7 @@ def tile_shiftedpatchtokenization_pb_t_kernel(tc, x, ln2_g, ln2_b, w2_words, w2_
         haar_pool = ctx.enter_context(tc.tile_pool(name="haar_pool", bufs=2))
         stat_pool = ctx.enter_context(tc.tile_pool(name="stat_pool", bufs=2))
         u_pool = ctx.enter_context(tc.tile_pool(name="u_pool", bufs=2))
-        z_pool = ctx.enter_context(tc.tile_pool(name="z_pool", bufs=3))
+        z_pool = ctx.enter_context(tc.tile_pool(name="z_pool", bufs=2))
         code_pool = ctx.enter_context(tc.tile_pool(name="code_pool", bufs=2))
         io_pool = ctx.enter_context(tc.tile_pool(name="io_pool", bufs=3))
         tok_pool = ctx.enter_context(tc.tile_pool(name="tok_pool", bufs=6))
@@ -53,6 +57,11 @@ def tile_shiftedpatchtokenization_pb_t_kernel(tc, x, ln2_g, ln2_b, w2_words, w2_
         x_body = x.rearrange("b c (q r) w -> b (c q) (r w)", q=4)
         tok_rows = tok.rearrange("b t n -> (b t) n").rearrange("(m s) n -> m s n", s=64)
         out_rows = out.rearrange("b t n -> (b t) n").rearrange("(m s) n -> m s n", s=64)
+
+        one = const.tile([P, 1], F32)
+        root = const.tile([P, 1], F32)
+        nc.gpsimd.memset(one[:], 1.0)
+        nc.scalar.activation(out=root[:], in_=one[:], func=ACT.Sqrt)
 
         ident = const.tile([P, P], F32)
         make_identity(nc, ident[:])
@@ -75,12 +84,8 @@ def tile_shiftedpatchtokenization_pb_t_kernel(tc, x, ln2_g, ln2_b, w2_words, w2_
 
         gain_bf = const.tile([P, PASSES, 4], BF16)
         bias_bf = const.tile([P, PASSES, 4], BF16)
-        nc.sync.dma_start(out=gain_bf[:], in_=ln2_g.rearrange("(g p t) -> p g t", g=PASSES, p=P, t=4))
-        nc.sync.dma_start(out=bias_bf[:], in_=ln2_b.rearrange("(g p t) -> p g t", g=PASSES, p=P, t=4))
         gain = const.tile([P, PASSES, 4], F32)
         bias = const.tile([P, PASSES, 4], F32)
-        nc.vector.tensor_copy(out=gain[:], in_=gain_bf[:])
-        nc.vector.tensor_copy(out=bias[:], in_=bias_bf[:])
 
         quad_sums = const.tile([P, 2, 2 * BANDS, QUAD_PITCH], F32)
         nc.vector.memset(quad_sums[:], 0.0)
@@ -90,6 +95,10 @@ def tile_shiftedpatchtokenization_pb_t_kernel(tc, x, ln2_g, ln2_b, w2_words, w2_
         b2_all = const.tile([P, DIM], BF16)
 
         def load_weights():
+            nc.sync.dma_start(out=gain_bf[:], in_=ln2_g.rearrange("(g p t) -> p g t", g=PASSES, p=P, t=4))
+            nc.sync.dma_start(out=bias_bf[:], in_=ln2_b.rearrange("(g p t) -> p g t", g=PASSES, p=P, t=4))
+            nc.vector.tensor_copy(out=gain[:], in_=gain_bf[:])
+            nc.vector.tensor_copy(out=bias[:], in_=bias_bf[:])
             nc.vector.memset(w_scales[:].bitcast(I32), 0)
             for quadrant in range(4):
                 nc.sync.dma_start(
@@ -121,9 +130,10 @@ def tile_shiftedpatchtokenization_pb_t_kernel(tc, x, ln2_g, ln2_b, w2_words, w2_
             return xt[:].rearrange("p (r v) (w h) -> p r v w h", v=2, h=2)
 
         def detail_on_vector(blocks, dests):
-            rest = haar_pool.tile([P, BAND_ROWS, 128], F32, name="rest")
-            nc.vector.tensor_tensor(out=rest[:], in0=blocks[:, :, 1, :, 0], in1=blocks[:, :, 1, :, 1], op=ALU.add)
-            nc.vector.tensor_tensor(out=rest[:], in0=rest[:], in1=blocks[:, :, 0, :, 1], op=ALU.add)
+            rest_tile = haar_pool.tile([P, BAND_ROWS, 128], F32, name="rest")
+            rest = rest_tile[:, 0 : blocks.shape[1], :]
+            nc.vector.tensor_tensor(out=rest, in0=blocks[:, :, 1, :, 0], in1=blocks[:, :, 1, :, 1], op=ALU.add)
+            nc.vector.tensor_tensor(out=rest, in0=rest, in1=blocks[:, :, 0, :, 1], op=ALU.add)
             for dest, r0, count in dests:
                 nc.vector.scalar_tensor_tensor(
                     out=dest, in0=blocks[:, r0 : r0 + count, 0, :, 0], scalar=3.0, in1=rest[:, r0 : r0 + count, :],
@@ -142,35 +152,76 @@ def tile_shiftedpatchtokenization_pb_t_kernel(tc, x, ln2_g, ln2_b, w2_words, w2_
                 )
             nc.scalar.copy(out=dest, in_=detail[:])
 
-        def square_sums(halves, rows):
+        def square_sums_steps(halves, rows):
             bn = stat_pool.tile([P, 2, 16, 6], F32, name="bn")
-            for yq, (band, row) in enumerate(halves):
-                for xp in range(16):
+
+            def count(yq, first):
+                band, row = halves[yq]
+                for xp in range(first, first + 8):
                     nc.vector.bn_stats(
                         out=bn[:, yq, xp, :],
                         in_=band[:, :, row : row + 4, 4 + 8 * xp : 12 + 8 * xp].rearrange(
                             "p l r (c s) -> p l r s c", c=2
                         ),
                     )
-            squares = stat_pool.tile([P, 2, 16, 2], F32, name="squares")
-            nc.vector.tensor_tensor(out=squares[:], in0=bn[:, :, :, 1:6:3], in1=bn[:, :, :, 1:6:3], op=ALU.mult)
-            nc.vector.tensor_copy(
-                out=quad_sums[:, 0, rows, 1:33].rearrange("p y (x c) -> p y x c", c=2), in_=bn[:, :, :, 1:6:3]
-            )
-            nc.vector.scalar_tensor_tensor(
-                out=quad_sums[:, 1, rows, 1:33].rearrange("p y (x c) -> p y x c", c=2),
-                in0=squares[:], scalar=64.0, in1=bn[:, :, :, 2:6:3], op0=ALU.mult, op1=ALU.add,
-            )
 
-        def haar_band(kb, tensor_planes):
+            def count_and_file():
+                count(1, 8)
+                squares = stat_pool.tile([P, 2, 16, 2], F32, name="squares")
+                nc.vector.tensor_tensor(out=squares[:], in0=bn[:, :, :, 1:6:3], in1=bn[:, :, :, 1:6:3], op=ALU.mult)
+                nc.vector.tensor_copy(
+                    out=quad_sums[:, 0, rows, 1:33].rearrange("p y (x c) -> p y x c", c=2), in_=bn[:, :, :, 1:6:3]
+                )
+                nc.vector.scalar_tensor_tensor(
+                    out=quad_sums[:, 1, rows, 1:33].rearrange("p y (x c) -> p y x c", c=2),
+                    in0=squares[:], scalar=64.0, in1=bn[:, :, :, 2:6:3], op0=ALU.mult, op1=ALU.add,
+                )
+
+            return [lambda: count(0, 0), lambda: count(0, 8), lambda: count(1, 0), count_and_file]
+
+        def square_sums(halves, rows):
+            for step in square_sums_steps(halves, rows):
+                step()
+
+        def haar_band_steps(kb, tensor_planes):
             band = new_band(kb)
-            for l in range(PLANES):
+
+            def plane_step(l):
                 blocks = load_x(l, ((0, 16 * kb - 8, 16),))
-                if l in tensor_planes:
-                    detail_on_tensor(blocks, 0, band[:, l, 0:4, 4 : PADDED - 4])
-                    detail_on_tensor(blocks, 4, band[:, l, 4:8, 4 : PADDED - 4])
-                else:
-                    detail_on_vector(blocks, ((band[:, l, :, 4 : PADDED - 4], 0, BAND_ROWS),))
+
+                def make():
+                    if l in tensor_planes:
+                        detail_on_tensor(blocks, 0, band[:, l, 0:4, 4 : PADDED - 4])
+                        detail_on_tensor(blocks, 4, band[:, l, 4:8, 4 : PADDED - 4])
+                    else:
+                        detail_on_vector(blocks, ((band[:, l, :, 4 : PADDED - 4], 0, BAND_ROWS),))
+
+                return make
+
+            steps = [plane_step(l) for l in range(PLANES)]
+            return steps + square_sums_steps(((band, 0), (band, 4)), slice(2 * kb, 2 * kb + 2))
+
+        def haar_band_by_halves(kb, tensor_planes):
+            band = new_band(kb)
+            tiles = []
+            for l in range(PLANES):
+                xt = x_pool.tile([P, 2 * BAND_ROWS, 256], BF16, name="xt")
+                tiles.append(xt)
+            for half in range(2):
+                first = 16 * kb - 8 + 8 * half
+                for l in range(PLANES):
+                    nc.sync.dma_start(
+                        out=tiles[l][:, 8 * half : 8 * half + 8, :].rearrange("p r w -> p (r w)"),
+                        in_=x_body[:, 8 * l : 8 * l + 8, first * 256 : (first + 8) * 256],
+                    )
+            for half in range(2):
+                for l in range(PLANES):
+                    blocks = tiles[l][:].rearrange("p (r v) (w h) -> p r v w h", v=2, h=2)
+                    dest = band[:, l, 4 * half : 4 * half + 4, 4 : PADDED - 4]
+                    if l in tensor_planes:
+                        detail_on_tensor(blocks, 4 * half, dest)
+                    else:
+                        detail_on_vector(blocks[:, 4 * half : 4 * half + 4], ((dest, 0, 4),))
             square_sums(((band, 0), (band, 4)), slice(2 * kb, 2 * kb + 2))
 
         def haar_edges(tensor_planes):
@@ -195,7 +246,7 @@ def tile_shiftedpatchtokenization_pb_t_kernel(tc, x, ln2_g, ln2_b, w2_words, w2_
                 nc.sync.dma_start(out=bottom[q - 1 : P : 4, :, 4:8, :], in_=top[q:P:4, :, 4:8, :])
                 nc.sync.dma_start(out=quad_sums[q - 1 : P : 4, :, 9, :], in_=quad_sums[q:P:4, :, 1, :])
 
-        def token_stats(i):
+        def token_sums(i):
             inner = stat_pool.tile([P, 2, 34], F32, name="inner")
             outer = stat_pool.tile([P, 2, 34], F32, name="outer")
             nc.vector.tensor_tensor(
@@ -211,6 +262,9 @@ def tile_shiftedpatchtokenization_pb_t_kernel(tc, x, ln2_g, ln2_b, w2_words, w2_
             nc.vector.tensor_tensor(out=sums[:], in0=inner[:, :, 1:33:2], in1=inner[:, :, 2:34:2], op=ALU.add)
             nc.vector.tensor_tensor(out=edge[:], in0=outer[:, :, 0:32:2], in1=outer[:, :, 3:34:2], op=ALU.add)
             nc.vector.tensor_tensor(out=sums[:], in0=sums[:], in1=edge[:], op=ALU.add)
+            return sums
+
+        def token_stats(sums):
             both = psum_t.tile([P, 32], F32, name="turned")
             nc.tensor.matmul(out=both[:], lhsT=pair[:], rhs=sums[:].rearrange("p s j -> p (s j)"), start=True, stop=True)
             mean = stat_pool.tile([P, 16], F32, name="mean")
@@ -244,27 +298,74 @@ def tile_shiftedpatchtokenization_pb_t_kernel(tc, x, ln2_g, ln2_b, w2_words, w2_
                     out=dst, in_=src, func=ACT.Identity, bias=shift[:, j : j + 1], scale=rstd[:, j : j + 1]
                 )
 
-        def multiply(group, jp):
+        def multiply_pass(group, jp, g, acc):
             cols = slice(P * jp, P * jp + P)
-            acc = psum_mx.tile([P, DIM], F32, name="acc")
-            for g in range(PASSES):
-                nc.tensor.matmul_mx(
-                    out=acc[:],
-                    lhsT=group["codes"][:, g, cols].bitcast(FP8X4),
-                    lhsT_scale=group["scales"][:, g, cols],
-                    rhs=w_codes[:, g, :].bitcast(FP8X4),
-                    rhs_scale=w_scales[:, g, :],
-                    start=(g == 0),
-                    stop=(g == PASSES - 1),
-                )
+            nc.tensor.matmul_mx(
+                out=acc[:],
+                lhsT=group["codes"][:, g, cols].bitcast(FP8X4),
+                lhsT_scale=group["scales"][:, g, cols],
+                rhs=w_codes[:, g, :].bitcast(FP8X4),
+                rhs_scale=w_scales[:, g, :],
+                start=(g == 0),
+                stop=(g == PASSES - 1),
+            )
+
+        def add_and_store(group, jp, acc):
             s0 = group["s0"] + 2 * jp
             result = io_pool.tile([P, DIM], F32, name="result")
             nc.vector.tensor_tensor(out=result[:], in0=acc[:], in1=group["tok"][jp][:], op=ALU.add)
             nc.sync.dma_start(out=out_rows[:, s0 : s0 + 2, :], in_=result[:])
 
-        def patch_group(i, jc, stats, before):
+        def multiply(group, jp):
+            acc = psum_mx.tile([P, DIM], F32, name="acc")
+            for g in range(PASSES):
+                multiply_pass(group, jp, g, acc)
+            add_and_store(group, jp, acc)
+
+        def multiply_last(group):
+            accs = []
+            for jp in range(2):
+                acc = psum_mx.tile([P, DIM], F32, name="acc")
+                accs.append(acc)
+            for g in range(PASSES):
+                for jp in range(2):
+                    multiply_pass(group, jp, g, accs[jp])
+            for jp in range(2):
+                add_and_store(group, jp, accs[jp])
+
+        def open_group(n):
+            i, jc = divmod(n, GROUPS)
+            u = u_pool.tile([P, GROUP, WORDS], F32, name="u")
+            return {"n": n, "i": i, "jc": jc, "u": u, "vector_patches": FIRST_VECTOR_PATCHES if n == 0 else VECTOR_PATCHES[i]}
+
+        def fill_patch(group, jl):
+            i = group["i"]
             upper = bands[i]
             lower = bands[i + 1]
+            j = GROUP * group["jc"] + jl
+            on_vector = jl >= GROUP - group["vector_patches"]
+            uv = group["u"][:, jl, :].rearrange("p (a b c l) -> p a b c l", a=8, b=8, c=5, l=PLANES)
+            x0 = 8 * j
+            normalise(
+                uv[:, 0:4, :, 0, :], upper[:, :, 4:8, x0 + 4 : x0 + 12].rearrange("p l a b -> p a b l"),
+                stats[i], j, on_vector,
+            )
+            normalise(
+                uv[:, 4:8, :, 0, :], lower[:, :, 0:4, x0 + 4 : x0 + 12].rearrange("p l a b -> p a b l"),
+                stats[i], j, on_vector,
+            )
+            for sy, band in enumerate((upper, lower)):
+                for sx in range(2):
+                    normalise(
+                        uv[:, :, :, 1 + 2 * sy + sx, :],
+                        band[:, :, :, x0 + 8 * sx : x0 + 8 * sx + 8].rearrange("p l a b -> p a b l"),
+                        stats[i], j, on_vector,
+                    )
+
+        def patch_group(group, following, before):
+            i = group["i"]
+            jc = group["jc"]
+            u = group["u"]
             tok_tiles = []
             for jp in range(2):
                 s0 = 16 * i + GROUP * jc + 2 * jp
@@ -274,70 +375,85 @@ def tile_shiftedpatchtokenization_pb_t_kernel(tc, x, ln2_g, ln2_b, w2_words, w2_
                 nc.gpsimd.tensor_tensor(out=tok_b2[:], in0=tok_bf[:], in1=b2_all[:], op=ALU.add)
                 tok_tiles.append(tok_b2)
 
-            u = u_pool.tile([P, GROUP, WORDS], F32, name="u")
-            for jl in range(GROUP):
-                j = GROUP * jc + jl
-                on_vector = jl >= GROUP - VECTOR_PATCHES[i]
-                uv = u[:, jl, :].rearrange("p (a b c l) -> p a b c l", a=8, b=8, c=5, l=PLANES)
-                x0 = 8 * j
-                normalise(
-                    uv[:, 0:4, :, 0, :], upper[:, :, 4:8, x0 + 4 : x0 + 12].rearrange("p l a b -> p a b l"),
-                    stats, j, on_vector,
-                )
-                normalise(
-                    uv[:, 4:8, :, 0, :], lower[:, :, 0:4, x0 + 4 : x0 + 12].rearrange("p l a b -> p a b l"),
-                    stats, j, on_vector,
-                )
-                for sy, band in enumerate((upper, lower)):
-                    for sx in range(2):
-                        normalise(
-                            uv[:, :, :, 1 + 2 * sy + sx, :],
-                            band[:, :, :, x0 + 8 * sx : x0 + 8 * sx + 8].rearrange("p l a b -> p a b l"),
-                            stats, j, on_vector,
-                        )
-
             z_codes = code_pool.tile([P, PASSES, GROUP * 64], U32, name="z_codes", align_bytes=64)
             z_scales = code_pool.tile([P, PASSES, GROUP * 64], U8, name="z_scales", align_bytes=64)
-            for g in range(PASSES):
-                planes = z_pool.tile([P, 4, GROUP * 64], BF16, name="planes")
-                for ca in range(2):
-                    turned = psum_t.tile([P, GROUP, P], F32, name="turned")
-                    for jl in range(GROUP):
-                        nc.tensor.transpose(
-                            out=turned[:, jl, :], in_=u[:, jl, 256 * g + ca : 256 * (g + 1) : 2], identity=perm[:]
-                        )
-                    for cb in range(2):
-                        t = 2 * ca + cb
-                        nc.scalar.activation(
-                            out=planes[:, t, :].rearrange("p (jp m jj) -> p jp m jj", jp=2, m=64, jj=2),
-                            in_=turned[:, :, 64 * cb : 64 * cb + 64].rearrange("p (jp jj) m -> p jp m jj", jj=2),
-                            func=ACT.Identity,
-                            bias=bias[:, g, t : t + 1],
-                            scale=gain[:, g, t : t + 1],
-                        )
-                grouped = z_pool.tile([P, 4 * GROUP * 64], BF16, name="grouped", align_bytes=64)
+            for unit in COPY_UNITS:
+                count = len(unit)
+                planes = z_pool.tile([P, 4, 2 * GROUP * 64], BF16, name="planes")
+                for slot, g in enumerate(unit):
+                    step = todo.get((group["n"], g))
+                    if step is not None:
+                        step()
+                    if following is not None and g < GROUP:
+                        fill_patch(following, g)
+                    for ca in range(2):
+                        turned = psum_t.tile([P, GROUP, P], F32, name="turned")
+                        for jl in range(GROUP):
+                            nc.tensor.transpose(
+                                out=turned[:, jl, :], in_=u[:, jl, 256 * g + ca : 256 * (g + 1) : 2], identity=perm[:]
+                            )
+                        for cb in range(2):
+                            t = 2 * ca + cb
+                            nc.scalar.activation(
+                                out=planes[:, t, GROUP * 64 * slot : GROUP * 64 * (slot + 1)].rearrange(
+                                    "p (jp m jj) -> p jp m jj", jp=2, m=64, jj=2
+                                ),
+                                in_=turned[:, :, 64 * cb : 64 * cb + 64].rearrange("p (jp jj) m -> p jp m jj", jj=2),
+                                func=ACT.Identity,
+                                bias=bias[:, g, t : t + 1],
+                                scale=gain[:, g, t : t + 1],
+                            )
+                    if before is not None and g in MULTIPLY_BEHIND:
+                        multiply(before, MULTIPLY_BEHIND.index(g))
+                passes = slice(unit[0], unit[0] + count)
+                grouped = z_pool.tile([P, 2 * 4 * GROUP * 64], BF16, name="grouped", align_bytes=64)
                 nc.vector.tensor_copy(
-                    out=grouped[:].rearrange("p (c i t) -> p c t i", i=4, t=4),
-                    in_=planes[:].rearrange("p t (c i) -> p c t i", i=4),
+                    out=grouped[:, 0 : count * 4 * GROUP * 64].rearrange("p (c i t) -> p c t i", i=4, t=4),
+                    in_=planes[:, :, 0 : count * GROUP * 64].rearrange("p t (c i) -> p c t i", i=4),
                 )
-                nc.vector.quantize_mx(out=z_codes[:, g, :].bitcast(FP8X4), scales=z_scales[:, g, :], in_=grouped[:])
-                if before is not None and g in MULTIPLY_BEHIND:
-                    multiply(before, MULTIPLY_BEHIND.index(g))
+                nc.vector.quantize_mx(
+                    out=z_codes[:, passes, :].rearrange("p g c -> p (g c)").bitcast(FP8X4),
+                    scales=z_scales[:, passes, :].rearrange("p g c -> p (g c)"),
+                    in_=grouped[:, 0 : count * 4 * GROUP * 64],
+                )
 
             return {"codes": z_codes, "scales": z_scales, "tok": tok_tiles, "s0": 16 * i + GROUP * jc}
 
+        stats = {}
+        row_sums = {}
+        todo = {}
+
+        def sums_step(i):
+            def make():
+                row_sums[i] = token_sums(i)
+
+            return make
+
+        def stats_step(i):
+            def make():
+                stats[i] = token_stats(row_sums[i])
+
+            return make
+
         with tc.manual_schedule(engines={mybir.EngineType.PE}):
             haar_edges(HEAD_TENSOR_PLANES)
-            haar_band(1, HEAD_TENSOR_PLANES)
+            haar_band_by_halves(1, HEAD_TENSOR_PLANES)
             load_weights()
-            stats = {0: token_stats(0)}
+            stats[0] = token_stats(token_sums(0))
+            for i in range(1, TOKEN_ROWS):
+                todo[(GROUPS * (i - 1) + STATS_AT[0], STATS_AT[1])] = stats_step(i)
+            group = open_group(0)
+            for jl in range(GROUP):
+                fill_patch(group, jl)
             before = None
-            for i in range(TOKEN_ROWS):
-                if i + 2 < BANDS - 1:
-                    haar_band(i + 2, ())
-                for jc in range(GROUPS):
-                    if jc == GROUPS - 1 and i + 1 < TOKEN_ROWS:
-                        stats[i + 1] = token_stats(i + 1)
-                    before = patch_group(i, jc, stats[i], before)
-            for jp in range(2):
-                multiply(before, jp)
+            for n in range(TOKEN_ROWS * GROUPS):
+                i, jc = divmod(n, GROUPS)
+                if jc == 0 and i + 2 < BANDS - 1:
+                    steps = haar_band_steps(i + 2, LATER_TENSOR_PLANES[i])
+                    steps.extend([sums_step(row) for row in range(i + 1, TOKEN_ROWS if i + 2 == BANDS - 2 else i + 2)])
+                    for k, step in enumerate(steps):
+                        todo[(n + k // PASSES, k % PASSES)] = step
+                following = open_group(n + 1) if n + 1 < TOKEN_ROWS * GROUPS else None
+                before = patch_group(group, following, before)
+                group = following
+            multiply_last(before)

@@ -18,19 +18,21 @@ DIM = 512
 K = 2560
 PASSES = K // 512
 EPS = 1e-5
+PHASES = 4
+IMAGES = BATCH // PHASES
+STRIPS = 16
+SHIFT = P // STRIPS
 PLANES = 4
 BAND_ROWS = 8
-BANDS = 5
 PADDED = 136
-QUAD_PITCH = 36
-TOKEN_ROWS = 4
+QUAD_PITCH = 34
 GROUP = 4
 GROUPS = 16 // GROUP
 WORDS = K // 2
-VECTOR_PATCHES = (1, 1, 3, 3)
+VECTOR_PATCHES = ((2, 1), (2, 1), (2, 1), (3, 3))
 FIRST_VECTOR_PATCHES = 3
-HEAD_TENSOR_PLANES = (1, 3)
-LATER_TENSOR_PLANES = ((1, 3), (1,))
+TENSOR_PLANES = ((1, 3), (1, 3), (1, 3), (1,))
+SUMS_BEHIND = 1
 STATS_AT = (2, 3)
 COPY_UNITS = ((0, 1), (2, 3), (4,))
 MULTIPLY_BEHIND = (2, 4)
@@ -43,7 +45,6 @@ def tile_shiftedpatchtokenization_pb_t_kernel(tc, x, ln2_g, ln2_b, w2_words, w2_
     with ExitStack() as ctx:
         const = ctx.enter_context(tc.tile_pool(name="const", bufs=1))
         x_pool = ctx.enter_context(tc.tile_pool(name="x_pool", bufs=6))
-        band_pool = ctx.enter_context(tc.tile_pool(name="band_pool", bufs=4))
         haar_pool = ctx.enter_context(tc.tile_pool(name="haar_pool", bufs=2))
         stat_pool = ctx.enter_context(tc.tile_pool(name="stat_pool", bufs=2))
         u_pool = ctx.enter_context(tc.tile_pool(name="u_pool", bufs=2))
@@ -54,28 +55,56 @@ def tile_shiftedpatchtokenization_pb_t_kernel(tc, x, ln2_g, ln2_b, w2_words, w2_
         psum_t = ctx.enter_context(tc.psum_pool(name="psum_t", bufs=5))
         psum_mx = ctx.enter_context(tc.psum_pool(name="psum_mx", bufs=3))
 
-        x_body = x.rearrange("b c (q r) w -> b (c q) (r w)", q=4)
-        tok_rows = tok.rearrange("b t n -> (b t) n").rearrange("(m s) n -> m s n", s=64)
-        out_rows = out.rearrange("b t n -> (b t) n").rearrange("(m s) n -> m s n", s=64)
+        x_rows = x.rearrange("(f b) k (s r) w -> f k s b (r w)", f=PHASES, s=STRIPS)
+        tok_rows = tok.rearrange("b t n -> (b t) n").rearrange("(f m j) n -> f m j n", f=PHASES, j=16)
+        out_rows = out.rearrange("b t n -> (b t) n").rearrange("(f m j) n -> f m j n", f=PHASES, j=16)
 
         one = const.tile([P, 1], F32)
+        zero = const.tile([P, 1], F32)
         root = const.tile([P, 1], F32)
         nc.gpsimd.memset(one[:], 1.0)
+        nc.gpsimd.memset(zero[:], 0.0)
         nc.scalar.activation(out=root[:], in_=one[:], func=ACT.Sqrt)
+
+        band_sets = []
+        quad_sets = []
+        for half in range(2):
+            upper = const.tile([P, PLANES, BAND_ROWS, PADDED], F32, name="upper%d" % half)
+            lower = const.tile([P, PLANES, BAND_ROWS, PADDED], F32, name="lower%d" % half)
+            quads = const.tile([P, 2, 2, QUAD_PITCH], F32, name="quads%d" % half)
+            band_sets.append((upper, lower))
+            quad_sets.append(quads)
+
+        def clear_set(half):
+            upper, lower = band_sets[half]
+            nc.scalar.copy(out=upper[:, :, 0:4, :], in_=zero[:, 0:1].to_broadcast([P, PLANES, 4, PADDED]))
+            nc.scalar.copy(out=lower[:, :, 4:8, :], in_=zero[:, 0:1].to_broadcast([P, PLANES, 4, PADDED]))
+            for own in (upper[:, :, 4:8, :], lower[:, :, 0:4, :]):
+                nc.vector.memset(own[:, :, :, 0:4], 0.0)
+                nc.vector.memset(own[:, :, :, PADDED - 4 : PADDED], 0.0)
+            nc.vector.memset(quad_sets[half][:], 0.0)
+
+        clear_set(0)
 
         ident = const.tile([P, P], F32)
         make_identity(nc, ident[:])
-        ident_bcq = ident[:].rearrange("p (b c q) -> p b c q", b=BATCH, c=2, q=4)
         perm = const.tile([P, P], F32)
         nc.vector.tensor_copy(
-            out=perm[:].rearrange("p (c b q) -> p c b q", c=2, b=BATCH, q=4),
-            in_=ident[:].rearrange("p (b c q) -> p c b q", b=BATCH, c=2, q=4),
+            out=perm[:].rearrange("p (c b s) -> p c b s", c=2, b=IMAGES, s=STRIPS),
+            in_=ident[:].rearrange("p (s b c) -> p c b s", c=2, b=IMAGES, s=STRIPS),
         )
         pair = const.tile([P, P], F32)
-        pair_bcq = pair[:].rearrange("p (b c q) -> p b c q", b=BATCH, c=2, q=4)
-        nc.vector.tensor_copy(out=pair_bcq[:, :, 0, :], in_=ident_bcq[:, :, 1, :])
-        nc.vector.tensor_copy(out=pair_bcq[:, :, 1, :], in_=ident_bcq[:, :, 0, :])
+        pair_kc = pair[:].rearrange("p (k c) -> p k c", c=2)
+        ident_kc = ident[:].rearrange("p (k c) -> p k c", c=2)
+        nc.vector.tensor_copy(out=pair_kc[:, :, 0], in_=ident_kc[:, :, 1])
+        nc.vector.tensor_copy(out=pair_kc[:, :, 1], in_=ident_kc[:, :, 0])
         nc.vector.tensor_tensor(out=pair[:], in0=pair[:], in1=ident[:], op=ALU.add)
+        from_above = const.tile([P, P], F32)
+        from_below = const.tile([P, P], F32)
+        nc.vector.memset(from_above[:, 0:SHIFT], 0.0)
+        nc.vector.tensor_copy(out=from_above[:, SHIFT:P], in_=pair[:, 0 : P - SHIFT])
+        nc.vector.memset(from_below[:, P - SHIFT : P], 0.0)
+        nc.vector.tensor_copy(out=from_below[:, 0 : P - SHIFT], in_=pair[:, SHIFT:P])
 
         three_eye = const.tile([P, P], BF16)
         minus_eye = const.tile([P, P], BF16)
@@ -86,9 +115,6 @@ def tile_shiftedpatchtokenization_pb_t_kernel(tc, x, ln2_g, ln2_b, w2_words, w2_
         bias_bf = const.tile([P, PASSES, 4], BF16)
         gain = const.tile([P, PASSES, 4], F32)
         bias = const.tile([P, PASSES, 4], F32)
-
-        quad_sums = const.tile([P, 2, 2 * BANDS, QUAD_PITCH], F32)
-        nc.vector.memset(quad_sums[:], 0.0)
 
         w_codes = const.tile([P, PASSES, DIM], U32, align_bytes=64)
         w_scales = const.tile([P, PASSES, DIM], U8, align_bytes=64)
@@ -111,22 +137,14 @@ def tile_shiftedpatchtokenization_pb_t_kernel(tc, x, ln2_g, ln2_b, w2_words, w2_
             )
             nc.sync.dma_start(out=b2_all[:], in_=b2.partition_broadcast(P))
 
-        bands = {}
-
-        def new_band(kb):
-            band = band_pool.tile([P, PLANES, BAND_ROWS, PADDED], F32, name="band")
-            bands[kb] = band
-            nc.vector.memset(band[:, :, :, 0:4], 0.0)
-            nc.vector.memset(band[:, :, :, PADDED - 4 : PADDED], 0.0)
-            return band
-
-        def load_x(l, loads):
-            xt = x_pool.tile([P, 2 * BAND_ROWS, 256], BF16, name="xt")
-            for at, first, count in loads:
+        def load_rows(xt, f, l, first, count):
+            for c in range(2):
                 nc.sync.dma_start(
-                    out=xt[:, at : at + count, :].rearrange("p r w -> p (r w)"),
-                    in_=x_body[:, 8 * l : 8 * l + 8, first * 256 : (first + count) * 256],
+                    out=xt[c:P:2, first : first + count, :].rearrange("p r w -> p (r w)"),
+                    in_=x_rows[f, 2 * l + c, :, :, first * 256 : (first + count) * 256],
                 )
+
+        def as_blocks(xt):
             return xt[:].rearrange("p (r v) (w h) -> p r v w h", v=2, h=2)
 
         def detail_on_vector(blocks, dests):
@@ -152,7 +170,14 @@ def tile_shiftedpatchtokenization_pb_t_kernel(tc, x, ln2_g, ln2_b, w2_words, w2_
                 )
             nc.scalar.copy(out=dest, in_=detail[:])
 
-        def square_sums_steps(halves, rows):
+        def own_rows(f, l):
+            upper, lower = band_sets[f % 2]
+            return upper[:, l, 4:8, 4 : PADDED - 4], lower[:, l, 0:4, 4 : PADDED - 4]
+
+        def square_sums_steps(f):
+            upper, lower = band_sets[f % 2]
+            quads = quad_sets[f % 2]
+            halves = ((upper, 4), (lower, 0))
             bn = stat_pool.tile([P, 2, 16, 6], F32, name="bn")
 
             def count(yq, first):
@@ -170,112 +195,100 @@ def tile_shiftedpatchtokenization_pb_t_kernel(tc, x, ln2_g, ln2_b, w2_words, w2_
                 squares = stat_pool.tile([P, 2, 16, 2], F32, name="squares")
                 nc.vector.tensor_tensor(out=squares[:], in0=bn[:, :, :, 1:6:3], in1=bn[:, :, :, 1:6:3], op=ALU.mult)
                 nc.vector.tensor_copy(
-                    out=quad_sums[:, 0, rows, 1:33].rearrange("p y (x c) -> p y x c", c=2), in_=bn[:, :, :, 1:6:3]
+                    out=quads[:, 0, :, 1:33].rearrange("p y (x c) -> p y x c", c=2), in_=bn[:, :, :, 1:6:3]
                 )
                 nc.vector.scalar_tensor_tensor(
-                    out=quad_sums[:, 1, rows, 1:33].rearrange("p y (x c) -> p y x c", c=2),
+                    out=quads[:, 1, :, 1:33].rearrange("p y (x c) -> p y x c", c=2),
                     in0=squares[:], scalar=64.0, in1=bn[:, :, :, 2:6:3], op0=ALU.mult, op1=ALU.add,
                 )
 
             return [lambda: count(0, 0), lambda: count(0, 8), lambda: count(1, 0), count_and_file]
 
-        def square_sums(halves, rows):
-            for step in square_sums_steps(halves, rows):
-                step()
+        def rows_from_below(f):
+            upper, lower = band_sets[f % 2]
+            nc.sync.dma_start(out=lower[0 : P - SHIFT, :, 4:8, :], in_=upper[SHIFT:P, :, 4:8, :])
 
-        def haar_band_steps(kb, tensor_planes):
-            band = new_band(kb)
+        def rows_from_above(f):
+            upper, lower = band_sets[f % 2]
+            nc.sync.dma_start(out=upper[SHIFT:P, :, 0:4, :], in_=lower[0 : P - SHIFT, :, 0:4, :])
 
+        def haar_steps(f):
             def plane_step(l):
-                blocks = load_x(l, ((0, 16 * kb - 8, 16),))
+                xt = x_pool.tile([P, 2 * BAND_ROWS, 256], BF16, name="xt")
+                load_rows(xt, f, l, 0, 2 * BAND_ROWS)
+                blocks = as_blocks(xt)
+                top, bottom = own_rows(f, l)
 
                 def make():
-                    if l in tensor_planes:
-                        detail_on_tensor(blocks, 0, band[:, l, 0:4, 4 : PADDED - 4])
-                        detail_on_tensor(blocks, 4, band[:, l, 4:8, 4 : PADDED - 4])
+                    if l in TENSOR_PLANES[f]:
+                        detail_on_tensor(blocks, 0, top)
+                        detail_on_tensor(blocks, 4, bottom)
                     else:
-                        detail_on_vector(blocks, ((band[:, l, :, 4 : PADDED - 4], 0, BAND_ROWS),))
+                        detail_on_vector(blocks, ((top, 0, 4), (bottom, 4, 4)))
+                    if l == PLANES - 1:
+                        rows_from_below(f)
+                        rows_from_above(f)
 
                 return make
 
             steps = [plane_step(l) for l in range(PLANES)]
-            return steps + square_sums_steps(((band, 0), (band, 4)), slice(2 * kb, 2 * kb + 2))
+            return steps + square_sums_steps(f)
 
-        def haar_band_by_halves(kb, tensor_planes):
-            band = new_band(kb)
+        def load_by_halves(f):
             tiles = []
             for l in range(PLANES):
                 xt = x_pool.tile([P, 2 * BAND_ROWS, 256], BF16, name="xt")
                 tiles.append(xt)
             for half in range(2):
-                first = 16 * kb - 8 + 8 * half
                 for l in range(PLANES):
-                    nc.sync.dma_start(
-                        out=tiles[l][:, 8 * half : 8 * half + 8, :].rearrange("p r w -> p (r w)"),
-                        in_=x_body[:, 8 * l : 8 * l + 8, first * 256 : (first + 8) * 256],
-                    )
+                    load_rows(tiles[l], f, l, 8 * half, 8)
+            return tiles
+
+        def haar_by_halves(f, tiles):
+            sums = square_sums_steps(f)
             for half in range(2):
                 for l in range(PLANES):
-                    blocks = tiles[l][:].rearrange("p (r v) (w h) -> p r v w h", v=2, h=2)
-                    dest = band[:, l, 4 * half : 4 * half + 4, 4 : PADDED - 4]
-                    if l in tensor_planes:
+                    blocks = as_blocks(tiles[l])
+                    dest = own_rows(f, l)[half]
+                    if l in TENSOR_PLANES[f]:
                         detail_on_tensor(blocks, 4 * half, dest)
                     else:
                         detail_on_vector(blocks[:, 4 * half : 4 * half + 4], ((dest, 0, 4),))
-            square_sums(((band, 0), (band, 4)), slice(2 * kb, 2 * kb + 2))
-
-        def haar_edges(tensor_planes):
-            top = new_band(0)
-            bottom = new_band(BANDS - 1)
-            nc.gpsimd.memset(top[:, :, 0:4, :], 0.0)
-            nc.gpsimd.memset(bottom[:, :, 4:8, :], 0.0)
-            for l in range(PLANES):
-                blocks = load_x(l, ((0, 0, 8), (8, 56, 8)))
-                if l in tensor_planes:
-                    detail_on_tensor(blocks, 0, top[:, l, 4:8, 4 : PADDED - 4])
-                    detail_on_tensor(blocks, 4, bottom[:, l, 0:4, 4 : PADDED - 4])
+                if half == 0:
+                    rows_from_below(f)
                 else:
-                    detail_on_vector(
-                        blocks, ((top[:, l, 4:8, 4 : PADDED - 4], 0, 4), (bottom[:, l, 0:4, 4 : PADDED - 4], 4, 4))
-                    )
-            square_sums(((top, 4), (bottom, 0)), slice(1, 9, 7))
-            for q in range(1, 4):
-                nc.sync.dma_start(out=top[q:P:4, :, 0:4, :], in_=bottom[q - 1 : P : 4, :, 0:4, :])
-                nc.sync.dma_start(out=quad_sums[q:P:4, :, 0, :], in_=quad_sums[q - 1 : P : 4, :, 8, :])
-            for q in range(1, 4):
-                nc.sync.dma_start(out=bottom[q - 1 : P : 4, :, 4:8, :], in_=top[q:P:4, :, 4:8, :])
-                nc.sync.dma_start(out=quad_sums[q - 1 : P : 4, :, 9, :], in_=quad_sums[q:P:4, :, 1, :])
+                    rows_from_above(f)
+                sums[2 * half]()
+                sums[2 * half + 1]()
 
-        def token_sums(i):
-            inner = stat_pool.tile([P, 2, 34], F32, name="inner")
-            outer = stat_pool.tile([P, 2, 34], F32, name="outer")
-            nc.vector.tensor_tensor(
-                out=inner[:], in0=quad_sums[:, :, 2 * i + 1, 0:34], in1=quad_sums[:, :, 2 * i + 2, 0:34], op=ALU.add
-            )
-            nc.vector.tensor_tensor(
-                out=outer[:], in0=quad_sums[:, :, 2 * i, 0:34], in1=quad_sums[:, :, 2 * i + 3, 0:34], op=ALU.add
-            )
-            nc.vector.tensor_tensor(out=outer[:], in0=outer[:], in1=inner[:], op=ALU.add)
-            nc.vector.tensor_tensor(out=inner[:], in0=inner[:], in1=outer[:], op=ALU.add)
-            sums = stat_pool.tile([P, 2, 16], F32, name="sums")
-            edge = stat_pool.tile([P, 2, 16], F32, name="edge")
-            nc.vector.tensor_tensor(out=sums[:], in0=inner[:, :, 1:33:2], in1=inner[:, :, 2:34:2], op=ALU.add)
-            nc.vector.tensor_tensor(out=edge[:], in0=outer[:, :, 0:32:2], in1=outer[:, :, 3:34:2], op=ALU.add)
-            nc.vector.tensor_tensor(out=sums[:], in0=sums[:], in1=edge[:], op=ALU.add)
-            return sums
+        def token_sums(f):
+            quads = quad_sets[f % 2]
+            middle = stat_pool.tile([P, 2, 2, 16], F32, name="middle")
+            wide = stat_pool.tile([P, 2, 2, 16], F32, name="wide")
+            twice = stat_pool.tile([P, 2, 2, 16], F32, name="twice")
+            nc.vector.tensor_tensor(out=middle[:], in0=quads[:, :, :, 1:33:2], in1=quads[:, :, :, 2:34:2], op=ALU.add)
+            nc.vector.tensor_tensor(out=wide[:], in0=quads[:, :, :, 0:32:2], in1=quads[:, :, :, 3:34:2], op=ALU.add)
+            nc.vector.tensor_tensor(out=wide[:], in0=wide[:], in1=middle[:], op=ALU.add)
+            nc.vector.tensor_tensor(out=twice[:], in0=wide[:], in1=middle[:], op=ALU.add)
+            return wide, twice
 
         def token_stats(sums):
-            both = psum_t.tile([P, 32], F32, name="turned")
-            nc.tensor.matmul(out=both[:], lhsT=pair[:], rhs=sums[:].rearrange("p s j -> p (s j)"), start=True, stop=True)
+            wide, twice = sums
+            both = psum_t.tile([P, 2, 16], F32, name="turned")
+            terms = ((pair, twice, 0), (pair, twice, 1), (from_above, wide, 1), (from_below, wide, 0))
+            for step, (giver, part, y) in enumerate(terms):
+                nc.tensor.matmul(
+                    out=both[:], lhsT=giver[:], rhs=part[:, :, y, :], start=(step == 0), stop=(step == len(terms) - 1)
+                )
             mean = stat_pool.tile([P, 16], F32, name="mean")
             var = stat_pool.tile([P, 16], F32, name="var")
             mean_sq = stat_pool.tile([P, 16], F32, name="mean_sq")
             std = stat_pool.tile([P, 16], F32, name="std")
             rstd = stat_pool.tile([P, 16], F32, name="rstd")
             shift = stat_pool.tile([P, 16], F32, name="shift")
-            nc.vector.tensor_scalar(out=mean[:], in0=both[:, 0:16], scalar1=64.0 / K, scalar2=None, op0=ALU.mult)
+            nc.vector.tensor_scalar(out=mean[:], in0=both[:, 0, :], scalar1=64.0 / K, scalar2=None, op0=ALU.mult)
             nc.vector.tensor_scalar(
-                out=var[:], in0=both[:, 16:32], scalar1=1.0 / K, scalar2=36.0 * EPS, op0=ALU.mult, op1=ALU.add
+                out=var[:], in0=both[:, 1, :], scalar1=1.0 / K, scalar2=36.0 * EPS, op0=ALU.mult, op1=ALU.add
             )
             nc.vector.tensor_tensor(out=mean_sq[:], in0=mean[:], in1=mean[:], op=ALU.mult)
             nc.vector.tensor_tensor(out=var[:], in0=var[:], in1=mean_sq[:], op=ALU.subtract)
@@ -311,10 +324,10 @@ def tile_shiftedpatchtokenization_pb_t_kernel(tc, x, ln2_g, ln2_b, w2_words, w2_
             )
 
         def add_and_store(group, jp, acc):
-            s0 = group["s0"] + 2 * jp
+            j0 = group["j0"] + 2 * jp
             result = io_pool.tile([P, DIM], F32, name="result")
             nc.vector.tensor_tensor(out=result[:], in0=acc[:], in1=group["tok"][jp][:], op=ALU.add)
-            nc.sync.dma_start(out=out_rows[:, s0 : s0 + 2, :], in_=result[:])
+            nc.sync.dma_start(out=out_rows[group["f"], :, j0 : j0 + 2, :], in_=result[:])
 
         def multiply(group, jp):
             acc = psum_mx.tile([P, DIM], F32, name="acc")
@@ -334,43 +347,42 @@ def tile_shiftedpatchtokenization_pb_t_kernel(tc, x, ln2_g, ln2_b, w2_words, w2_
                 add_and_store(group, jp, accs[jp])
 
         def open_group(n):
-            i, jc = divmod(n, GROUPS)
+            f, jc = divmod(n, GROUPS)
             u = u_pool.tile([P, GROUP, WORDS], F32, name="u")
-            return {"n": n, "i": i, "jc": jc, "u": u, "vector_patches": FIRST_VECTOR_PATCHES if n == 0 else VECTOR_PATCHES[i]}
+            return {"n": n, "f": f, "jc": jc, "u": u, "vector_patches": FIRST_VECTOR_PATCHES if n == 0 else VECTOR_PATCHES[f][n % 2]}
 
         def fill_patch(group, jl):
-            i = group["i"]
-            upper = bands[i]
-            lower = bands[i + 1]
+            f = group["f"]
+            upper, lower = band_sets[f % 2]
             j = GROUP * group["jc"] + jl
             on_vector = jl >= GROUP - group["vector_patches"]
             uv = group["u"][:, jl, :].rearrange("p (a b c l) -> p a b c l", a=8, b=8, c=5, l=PLANES)
             x0 = 8 * j
             normalise(
                 uv[:, 0:4, :, 0, :], upper[:, :, 4:8, x0 + 4 : x0 + 12].rearrange("p l a b -> p a b l"),
-                stats[i], j, on_vector,
+                stats[f], j, on_vector,
             )
             normalise(
                 uv[:, 4:8, :, 0, :], lower[:, :, 0:4, x0 + 4 : x0 + 12].rearrange("p l a b -> p a b l"),
-                stats[i], j, on_vector,
+                stats[f], j, on_vector,
             )
             for sy, band in enumerate((upper, lower)):
                 for sx in range(2):
                     normalise(
                         uv[:, :, :, 1 + 2 * sy + sx, :],
                         band[:, :, :, x0 + 8 * sx : x0 + 8 * sx + 8].rearrange("p l a b -> p a b l"),
-                        stats[i], j, on_vector,
+                        stats[f], j, on_vector,
                     )
 
         def patch_group(group, following, before):
-            i = group["i"]
+            f = group["f"]
             jc = group["jc"]
             u = group["u"]
             tok_tiles = []
             for jp in range(2):
-                s0 = 16 * i + GROUP * jc + 2 * jp
+                j0 = GROUP * jc + 2 * jp
                 tok_bf = io_pool.tile([P, DIM], BF16, name="tok_bf")
-                nc.sync.dma_start(out=tok_bf[:], in_=tok_rows[:, s0 : s0 + 2, :])
+                nc.sync.dma_start(out=tok_bf[:], in_=tok_rows[f, :, j0 : j0 + 2, :])
                 tok_b2 = tok_pool.tile([P, DIM], F32, name="tok_b2")
                 nc.gpsimd.tensor_tensor(out=tok_b2[:], in0=tok_bf[:], in1=b2_all[:], op=ALU.add)
                 tok_tiles.append(tok_b2)
@@ -417,43 +429,44 @@ def tile_shiftedpatchtokenization_pb_t_kernel(tc, x, ln2_g, ln2_b, w2_words, w2_
                     in_=grouped[:, 0 : count * 4 * GROUP * 64],
                 )
 
-            return {"codes": z_codes, "scales": z_scales, "tok": tok_tiles, "s0": 16 * i + GROUP * jc}
+            return {"codes": z_codes, "scales": z_scales, "tok": tok_tiles, "f": f, "j0": GROUP * jc}
 
         stats = {}
         row_sums = {}
         todo = {}
 
-        def sums_step(i):
+        def sums_step(f):
             def make():
-                row_sums[i] = token_sums(i)
+                row_sums[f] = token_sums(f)
 
             return make
 
-        def stats_step(i):
+        def stats_step(f):
             def make():
-                stats[i] = token_stats(row_sums[i])
+                stats[f] = token_stats(row_sums[f])
 
             return make
 
         with tc.manual_schedule(engines={mybir.EngineType.PE}):
-            haar_edges(HEAD_TENSOR_PLANES)
-            haar_band_by_halves(1, HEAD_TENSOR_PLANES)
+            first_tiles = load_by_halves(0)
             load_weights()
+            haar_by_halves(0, first_tiles)
+            clear_set(1)
             stats[0] = token_stats(token_sums(0))
-            for i in range(1, TOKEN_ROWS):
-                todo[(GROUPS * (i - 1) + STATS_AT[0], STATS_AT[1])] = stats_step(i)
             group = open_group(0)
             for jl in range(GROUP):
                 fill_patch(group, jl)
             before = None
-            for n in range(TOKEN_ROWS * GROUPS):
-                i, jc = divmod(n, GROUPS)
-                if jc == 0 and i + 2 < BANDS - 1:
-                    steps = haar_band_steps(i + 2, LATER_TENSOR_PLANES[i])
-                    steps.extend([sums_step(row) for row in range(i + 1, TOKEN_ROWS if i + 2 == BANDS - 2 else i + 2)])
+            for n in range(PHASES * GROUPS):
+                f, jc = divmod(n, GROUPS)
+                if jc == 0 and f + 1 < PHASES:
+                    steps = haar_steps(f + 1)
                     for k, step in enumerate(steps):
                         todo[(n + k // PASSES, k % PASSES)] = step
-                following = open_group(n + 1) if n + 1 < TOKEN_ROWS * GROUPS else None
+                    k = len(steps) - 1 + SUMS_BEHIND
+                    todo[(n + k // PASSES, k % PASSES)] = sums_step(f + 1)
+                    todo[(n + STATS_AT[0], STATS_AT[1])] = stats_step(f + 1)
+                following = open_group(n + 1) if n + 1 < PHASES * GROUPS else None
                 before = patch_group(group, following, before)
                 group = following
             multiply_last(before)

@@ -44,16 +44,16 @@ def tile_shiftedpatchtokenization_pb_t_kernel(tc, x, ln2_g, ln2_b, w2_words, w2_
     nc = tc.nc
     with ExitStack() as ctx:
         const = ctx.enter_context(tc.tile_pool(name="const", bufs=1))
-        x_pool = ctx.enter_context(tc.tile_pool(name="x_pool", bufs=6))
+        x_pool = ctx.enter_context(tc.tile_pool(name="x_pool", bufs=4))
         haar_pool = ctx.enter_context(tc.tile_pool(name="haar_pool", bufs=2))
         stat_pool = ctx.enter_context(tc.tile_pool(name="stat_pool", bufs=2))
         u_pool = ctx.enter_context(tc.tile_pool(name="u_pool", bufs=2))
-        z_pool = ctx.enter_context(tc.tile_pool(name="z_pool", bufs=2))
+        z_pool = ctx.enter_context(tc.tile_pool(name="z_pool", bufs=3))
         code_pool = ctx.enter_context(tc.tile_pool(name="code_pool", bufs=2))
         io_pool = ctx.enter_context(tc.tile_pool(name="io_pool", bufs=3))
         tok_pool = ctx.enter_context(tc.tile_pool(name="tok_pool", bufs=6))
-        psum_t = ctx.enter_context(tc.psum_pool(name="psum_t", bufs=5))
-        psum_mx = ctx.enter_context(tc.psum_pool(name="psum_mx", bufs=3))
+        psum_t = ctx.enter_context(tc.psum_pool(name="psum_t", bufs=6))
+        psum_mx = ctx.enter_context(tc.psum_pool(name="psum_mx", bufs=2))
 
         x_rows = x.rearrange("(f b) k (s r) w -> f k s b (r w)", f=PHASES, s=STRIPS)
         tok_rows = tok.rearrange("b t n -> (b t) n").rearrange("(f m j) n -> f m j n", f=PHASES, j=16)

@@ -31,11 +31,12 @@ GROUPS = 16 // GROUP
 WORDS = K // 2
 VECTOR_PATCHES = ((2, 1), (2, 1), (2, 1), (3, 3))
 FIRST_VECTOR_PATCHES = 3
-TENSOR_PLANES = ((1, 3), (1, 3), (1, 3), (1,))
+TENSOR_PLANES = ((1, 3), (1, 3), (1, 3), (1, 2, 3))
 SUMS_BEHIND = 1
 STATS_AT = (2, 3)
 COPY_UNITS = ((0, 1), (2, 3), (4,))
 MULTIPLY_BEHIND = (2, 4)
+LAG = 2
 
 FLOPS = 2 * BATCH * 256 * K * DIM
 
@@ -49,11 +50,11 @@ def tile_shiftedpatchtokenization_pb_t_kernel(tc, x, ln2_g, ln2_b, w2_words, w2_
         stat_pool = ctx.enter_context(tc.tile_pool(name="stat_pool", bufs=2))
         u_pool = ctx.enter_context(tc.tile_pool(name="u_pool", bufs=2))
         z_pool = ctx.enter_context(tc.tile_pool(name="z_pool", bufs=3))
-        code_pool = ctx.enter_context(tc.tile_pool(name="code_pool", bufs=2))
+        code_pool = ctx.enter_context(tc.tile_pool(name="code_pool", bufs=3))
         io_pool = ctx.enter_context(tc.tile_pool(name="io_pool", bufs=3))
         tok_pool = ctx.enter_context(tc.tile_pool(name="tok_pool", bufs=6))
-        psum_t = ctx.enter_context(tc.psum_pool(name="psum_t", bufs=6))
-        psum_mx = ctx.enter_context(tc.psum_pool(name="psum_mx", bufs=2))
+        psum_t = ctx.enter_context(tc.psum_pool(name="psum_t", bufs=5))
+        psum_mx = ctx.enter_context(tc.psum_pool(name="psum_mx", bufs=3))
 
         x_rows = x.rearrange("(f b) k (s r) w -> f k s b (r w)", f=PHASES, s=STRIPS)
         tok_rows = tok.rearrange("b t n -> (b t) n").rearrange("(f m j) n -> f m j n", f=PHASES, j=16)
@@ -108,6 +109,8 @@ def tile_shiftedpatchtokenization_pb_t_kernel(tc, x, ln2_g, ln2_b, w2_words, w2_
 
         three_eye = const.tile([P, P], BF16)
         minus_eye = const.tile([P, P], BF16)
+        eye = const.tile([P, P], BF16)
+        nc.vector.tensor_copy(out=eye[:], in_=ident[:])
         nc.vector.tensor_scalar(out=three_eye[:], in0=ident[:], scalar1=3.0, scalar2=None, op0=ALU.mult)
         nc.vector.tensor_scalar(out=minus_eye[:], in0=ident[:], scalar1=-1.0, scalar2=None, op0=ALU.mult)
 
@@ -147,16 +150,31 @@ def tile_shiftedpatchtokenization_pb_t_kernel(tc, x, ln2_g, ln2_b, w2_words, w2_
         def as_blocks(xt):
             return xt[:].rearrange("p (r v) (w h) -> p r v w h", v=2, h=2)
 
-        def detail_on_vector(blocks, dests):
-            rest_tile = haar_pool.tile([P, BAND_ROWS, 128], F32, name="rest")
-            rest = rest_tile[:, 0 : blocks.shape[1], :]
-            nc.vector.tensor_tensor(out=rest, in0=blocks[:, :, 1, :, 0], in1=blocks[:, :, 1, :, 1], op=ALU.add)
-            nc.vector.tensor_tensor(out=rest, in0=rest, in1=blocks[:, :, 0, :, 1], op=ALU.add)
-            for dest, r0, count in dests:
-                nc.vector.scalar_tensor_tensor(
-                    out=dest, in0=blocks[:, r0 : r0 + count, 0, :, 0], scalar=3.0, in1=rest[:, r0 : r0 + count, :],
-                    op0=ALU.mult, op1=ALU.subtract,
+        def detail_on_vector(jobs):
+            rests = []
+            for blocks, dests in jobs:
+                rest_tile = haar_pool.tile([P, BAND_ROWS, 128], F32, name="rest")
+                rests.append(rest_tile[:, 0 : blocks.shape[1], :])
+            for (blocks, dests), rest in zip(jobs, rests):
+                nc.vector.tensor_tensor(out=rest, in0=blocks[:, :, 1, :, 0], in1=blocks[:, :, 1, :, 1], op=ALU.add)
+            for (blocks, dests), rest in zip(jobs, rests):
+                nc.vector.tensor_tensor(out=rest, in0=rest, in1=blocks[:, :, 0, :, 1], op=ALU.add)
+            for (blocks, dests), rest in zip(jobs, rests):
+                for dest, r0, count in dests:
+                    nc.vector.scalar_tensor_tensor(
+                        out=dest, in0=blocks[:, r0 : r0 + count, 0, :, 0], scalar=3.0, in1=rest[:, r0 : r0 + count, :],
+                        op0=ALU.mult, op1=ALU.subtract,
+                    )
+
+        def rest_on_tensor(blocks, r0, dest):
+            rest = psum_t.tile([P, 4, P], F32, name="turned")
+            for step, (v, h) in enumerate(((0, 1), (1, 0), (1, 1))):
+                nc.tensor.matmul(
+                    out=rest[:], lhsT=eye[:], rhs=blocks[:, r0 : r0 + 4, v, :, h], start=(step == 0), stop=(step == 2)
                 )
+            nc.vector.scalar_tensor_tensor(
+                out=dest, in0=blocks[:, r0 : r0 + 4, 0, :, 0], scalar=3.0, in1=rest[:], op0=ALU.mult, op1=ALU.subtract
+            )
 
         def detail_on_tensor(blocks, r0, dest):
             detail = psum_t.tile([P, 4, P], F32, name="turned")
@@ -213,26 +231,34 @@ def tile_shiftedpatchtokenization_pb_t_kernel(tc, x, ln2_g, ln2_b, w2_words, w2_
             nc.sync.dma_start(out=upper[SHIFT:P, :, 0:4, :], in_=lower[0 : P - SHIFT, :, 0:4, :])
 
         def haar_steps(f):
-            def plane_step(l):
+            blocks = []
+            for l in range(PLANES):
                 xt = x_pool.tile([P, 2 * BAND_ROWS, 256], BF16, name="xt")
                 load_rows(xt, f, l, 0, 2 * BAND_ROWS)
-                blocks = as_blocks(xt)
-                top, bottom = own_rows(f, l)
+                blocks.append(as_blocks(xt))
 
+            def tensor_step(l):
                 def make():
-                    if l in TENSOR_PLANES[f]:
-                        detail_on_tensor(blocks, 0, top)
-                        detail_on_tensor(blocks, 4, bottom)
-                    else:
-                        detail_on_vector(blocks, ((top, 0, 4), (bottom, 4, 4)))
-                    if l == PLANES - 1:
-                        rows_from_below(f)
-                        rows_from_above(f)
+                    top, bottom = own_rows(f, l)
+                    rest_on_tensor(blocks[l], 0, top)
+                    rest_on_tensor(blocks[l], 4, bottom)
 
                 return make
 
-            steps = [plane_step(l) for l in range(PLANES)]
-            return steps + square_sums_steps(f)
+            def vector_step():
+                jobs = []
+                for l in range(PLANES):
+                    if l not in TENSOR_PLANES[f]:
+                        top, bottom = own_rows(f, l)
+                        jobs.append((blocks[l], ((top, 0, 4), (bottom, 4, 4))))
+                detail_on_vector(jobs)
+
+            def exchange_step():
+                rows_from_below(f)
+                rows_from_above(f)
+
+            tensor_steps = [tensor_step(l) for l in TENSOR_PLANES[f]]
+            return tensor_steps[0:1] + [vector_step] + tensor_steps[1:] + [exchange_step] + square_sums_steps(f)
 
         def load_by_halves(f):
             tiles = []
@@ -247,13 +273,15 @@ def tile_shiftedpatchtokenization_pb_t_kernel(tc, x, ln2_g, ln2_b, w2_words, w2_
         def haar_by_halves(f, tiles):
             sums = square_sums_steps(f)
             for half in range(2):
+                jobs = []
                 for l in range(PLANES):
                     blocks = as_blocks(tiles[l])
                     dest = own_rows(f, l)[half]
                     if l in TENSOR_PLANES[f]:
                         detail_on_tensor(blocks, 4 * half, dest)
                     else:
-                        detail_on_vector(blocks[:, 4 * half : 4 * half + 4], ((dest, 0, 4),))
+                        jobs.append((blocks[:, 4 * half : 4 * half + 4], ((dest, 0, 4),)))
+                detail_on_vector(jobs)
                 if half == 0:
                     rows_from_below(f)
                 else:
@@ -374,7 +402,18 @@ def tile_shiftedpatchtokenization_pb_t_kernel(tc, x, ln2_g, ln2_b, w2_words, w2_
                         stats[f], j, on_vector,
                     )
 
-        def patch_group(group, following, before):
+        pending = []
+
+        def quantise_pending():
+            for z_codes, z_scales, passes, grouped, count in pending:
+                nc.vector.quantize_mx(
+                    out=z_codes[:, passes, :].rearrange("p g c -> p (g c)").bitcast(FP8X4),
+                    scales=z_scales[:, passes, :].rearrange("p g c -> p (g c)"),
+                    in_=grouped[:, 0 : count * 4 * GROUP * 64],
+                )
+            pending.clear()
+
+        def patch_group(group, following, earlier):
             f = group["f"]
             jc = group["jc"]
             u = group["u"]
@@ -415,19 +454,16 @@ def tile_shiftedpatchtokenization_pb_t_kernel(tc, x, ln2_g, ln2_b, w2_words, w2_
                                 bias=bias[:, g, t : t + 1],
                                 scale=gain[:, g, t : t + 1],
                             )
-                    if before is not None and g in MULTIPLY_BEHIND:
-                        multiply(before, MULTIPLY_BEHIND.index(g))
+                    if earlier is not None and g in MULTIPLY_BEHIND:
+                        multiply(earlier, MULTIPLY_BEHIND.index(g))
                 passes = slice(unit[0], unit[0] + count)
                 grouped = z_pool.tile([P, 2 * 4 * GROUP * 64], BF16, name="grouped", align_bytes=64)
                 nc.vector.tensor_copy(
                     out=grouped[:, 0 : count * 4 * GROUP * 64].rearrange("p (c i t) -> p c t i", i=4, t=4),
                     in_=planes[:, :, 0 : count * GROUP * 64].rearrange("p t (c i) -> p c t i", i=4),
                 )
-                nc.vector.quantize_mx(
-                    out=z_codes[:, passes, :].rearrange("p g c -> p (g c)").bitcast(FP8X4),
-                    scales=z_scales[:, passes, :].rearrange("p g c -> p (g c)"),
-                    in_=grouped[:, 0 : count * 4 * GROUP * 64],
-                )
+                quantise_pending()
+                pending.append((z_codes, z_scales, passes, grouped, count))
 
             return {"codes": z_codes, "scales": z_scales, "tok": tok_tiles, "f": f, "j0": GROUP * jc}
 
@@ -456,7 +492,8 @@ def tile_shiftedpatchtokenization_pb_t_kernel(tc, x, ln2_g, ln2_b, w2_words, w2_
             group = open_group(0)
             for jl in range(GROUP):
                 fill_patch(group, jl)
-            before = None
+            made = {}
+            last = PHASES * GROUPS - 1
             for n in range(PHASES * GROUPS):
                 f, jc = divmod(n, GROUPS)
                 if jc == 0 and f + 1 < PHASES:
@@ -467,6 +504,10 @@ def tile_shiftedpatchtokenization_pb_t_kernel(tc, x, ln2_g, ln2_b, w2_words, w2_
                     todo[(n + k // PASSES, k % PASSES)] = sums_step(f + 1)
                     todo[(n + STATS_AT[0], STATS_AT[1])] = stats_step(f + 1)
                 following = open_group(n + 1) if n + 1 < PHASES * GROUPS else None
-                before = patch_group(group, following, before)
+                made[n] = patch_group(group, following, made.get(n - LAG))
                 group = following
-            multiply_last(before)
+            quantise_pending()
+            for n in range(last - LAG + 1, last):
+                for jp in range(2):
+                    multiply(made[n], jp)
+            multiply_last(made[last])

@@ -37,6 +37,7 @@ STATS_AT = (2, 3)
 COPY_UNITS = ((0, 1), (2, 3), (4,))
 MULTIPLY_BEHIND = (2, 4)
 LAG = 2
+CATCH_UP_BEHIND = (1, 2, 3, 4)
 
 FLOPS = 2 * BATCH * 256 * K * DIM
 
@@ -68,12 +69,13 @@ def tile_shiftedpatchtokenization_pb_t_kernel(tc, x, ln2_g, ln2_b, w2_words, w2_
         nc.scalar.activation(out=root[:], in_=one[:], func=ACT.Sqrt)
 
         band_sets = []
+        region_sets = []
         quad_sets = []
         for half in range(2):
-            upper = const.tile([P, PLANES, BAND_ROWS, PADDED], F32, name="upper%d" % half)
-            lower = const.tile([P, PLANES, BAND_ROWS, PADDED], F32, name="lower%d" % half)
+            region = const.tile([P, PLANES, 2 * BAND_ROWS, PADDED], F32, name="region%d" % half)
             quads = const.tile([P, 2, 2, QUAD_PITCH], F32, name="quads%d" % half)
-            band_sets.append((upper, lower))
+            band_sets.append((region[:, :, 0:BAND_ROWS, :], region[:, :, BAND_ROWS : 2 * BAND_ROWS, :]))
+            region_sets.append(region)
             quad_sets.append(quads)
 
         def clear_set(half):
@@ -249,8 +251,8 @@ def tile_shiftedpatchtokenization_pb_t_kernel(tc, x, ln2_g, ln2_b, w2_words, w2_
                 jobs = []
                 for l in range(PLANES):
                     if l not in TENSOR_PLANES[f]:
-                        top, bottom = own_rows(f, l)
-                        jobs.append((blocks[l], ((top, 0, 4), (bottom, 4, 4))))
+                        own = region_sets[f % 2][:, l, 4:12, 4 : PADDED - 4]
+                        jobs.append((blocks[l], ((own, 0, BAND_ROWS),)))
                 detail_on_vector(jobs)
 
             def exchange_step():
@@ -265,8 +267,9 @@ def tile_shiftedpatchtokenization_pb_t_kernel(tc, x, ln2_g, ln2_b, w2_words, w2_
             for l in range(PLANES):
                 xt = x_pool.tile([P, 2 * BAND_ROWS, 256], BF16, name="xt")
                 tiles.append(xt)
+            order = [l for l in range(PLANES) if l not in TENSOR_PLANES[f]] + list(TENSOR_PLANES[f])
             for half in range(2):
-                for l in range(PLANES):
+                for l in order:
                     load_rows(tiles[l], f, l, 8 * half, 8)
             return tiles
 
@@ -298,29 +301,30 @@ def tile_shiftedpatchtokenization_pb_t_kernel(tc, x, ln2_g, ln2_b, w2_words, w2_
             nc.vector.tensor_tensor(out=wide[:], in0=quads[:, :, :, 0:32:2], in1=quads[:, :, :, 3:34:2], op=ALU.add)
             nc.vector.tensor_tensor(out=wide[:], in0=wide[:], in1=middle[:], op=ALU.add)
             nc.vector.tensor_tensor(out=twice[:], in0=wide[:], in1=middle[:], op=ALU.add)
-            return wide, twice
+            own = stat_pool.tile([P, 2, 16], F32, name="own")
+            nc.vector.tensor_tensor(out=own[:], in0=twice[:, :, 0, :], in1=twice[:, :, 1, :], op=ALU.add)
+            return wide, own
 
         def token_stats(sums):
-            wide, twice = sums
+            wide, own = sums
             both = psum_t.tile([P, 2, 16], F32, name="turned")
-            terms = ((pair, twice, 0), (pair, twice, 1), (from_above, wide, 1), (from_below, wide, 0))
-            for step, (giver, part, y) in enumerate(terms):
-                nc.tensor.matmul(
-                    out=both[:], lhsT=giver[:], rhs=part[:, :, y, :], start=(step == 0), stop=(step == len(terms) - 1)
-                )
+            terms = ((from_above, wide[:, :, 1, :]), (from_below, wide[:, :, 0, :]), (pair, own[:]))
+            for step, (giver, part) in enumerate(terms):
+                nc.tensor.matmul(out=both[:], lhsT=giver[:], rhs=part, start=(step == 0), stop=(step == len(terms) - 1))
             mean = stat_pool.tile([P, 16], F32, name="mean")
             var = stat_pool.tile([P, 16], F32, name="var")
-            mean_sq = stat_pool.tile([P, 16], F32, name="mean_sq")
+            minus_sq = stat_pool.tile([P, 16], F32, name="minus_sq")
             std = stat_pool.tile([P, 16], F32, name="std")
             rstd = stat_pool.tile([P, 16], F32, name="rstd")
             shift = stat_pool.tile([P, 16], F32, name="shift")
             nc.vector.tensor_scalar(out=mean[:], in0=both[:, 0, :], scalar1=64.0 / K, scalar2=None, op0=ALU.mult)
-            nc.vector.tensor_scalar(
-                out=var[:], in0=both[:, 1, :], scalar1=1.0 / K, scalar2=36.0 * EPS, op0=ALU.mult, op1=ALU.add
+            nc.vector.scalar_tensor_tensor(
+                out=minus_sq[:], in0=mean[:], scalar=-1.0, in1=mean[:], op0=ALU.mult, op1=ALU.mult
             )
-            nc.vector.tensor_tensor(out=mean_sq[:], in0=mean[:], in1=mean[:], op=ALU.mult)
-            nc.vector.tensor_tensor(out=var[:], in0=var[:], in1=mean_sq[:], op=ALU.subtract)
-            nc.scalar.activation(out=std[:], in_=var[:], func=ACT.Sqrt)
+            nc.vector.scalar_tensor_tensor(
+                out=var[:], in0=both[:, 1, :], scalar=1.0 / K, in1=minus_sq[:], op0=ALU.mult, op1=ALU.add
+            )
+            nc.scalar.activation(out=std[:], in_=var[:], func=ACT.Sqrt, bias=36.0 * EPS)
             nc.vector.reciprocal(out=rstd[:], in_=std[:])
             nc.vector.scalar_tensor_tensor(
                 out=shift[:], in0=mean[:], scalar=-1.0, in1=rstd[:], op0=ALU.mult, op1=ALU.mult
@@ -387,11 +391,7 @@ def tile_shiftedpatchtokenization_pb_t_kernel(tc, x, ln2_g, ln2_b, w2_words, w2_
             uv = group["u"][:, jl, :].rearrange("p (a b c l) -> p a b c l", a=8, b=8, c=5, l=PLANES)
             x0 = 8 * j
             normalise(
-                uv[:, 0:4, :, 0, :], upper[:, :, 4:8, x0 + 4 : x0 + 12].rearrange("p l a b -> p a b l"),
-                stats[f], j, on_vector,
-            )
-            normalise(
-                uv[:, 4:8, :, 0, :], lower[:, :, 0:4, x0 + 4 : x0 + 12].rearrange("p l a b -> p a b l"),
+                uv[:, :, :, 0, :], region_sets[f % 2][:, :, 4:12, x0 + 4 : x0 + 12].rearrange("p l a b -> p a b l"),
                 stats[f], j, on_vector,
             )
             for sy, band in enumerate((upper, lower)):
@@ -454,8 +454,8 @@ def tile_shiftedpatchtokenization_pb_t_kernel(tc, x, ln2_g, ln2_b, w2_words, w2_
                                 bias=bias[:, g, t : t + 1],
                                 scale=gain[:, g, t : t + 1],
                             )
-                    if earlier is not None and g in MULTIPLY_BEHIND:
-                        multiply(earlier, MULTIPLY_BEHIND.index(g))
+                    if g in earlier:
+                        multiply(*earlier[g])
                 passes = slice(unit[0], unit[0] + count)
                 grouped = z_pool.tile([P, 2 * 4 * GROUP * 64], BF16, name="grouped", align_bytes=64)
                 nc.vector.tensor_copy(
@@ -504,10 +504,13 @@ def tile_shiftedpatchtokenization_pb_t_kernel(tc, x, ln2_g, ln2_b, w2_words, w2_
                     todo[(n + k // PASSES, k % PASSES)] = sums_step(f + 1)
                     todo[(n + STATS_AT[0], STATS_AT[1])] = stats_step(f + 1)
                 following = open_group(n + 1) if n + 1 < PHASES * GROUPS else None
-                made[n] = patch_group(group, following, made.get(n - LAG))
+                if n == last:
+                    earlier = dict(zip(CATCH_UP_BEHIND, [(made[m], jp) for m in range(last - LAG, last) for jp in range(2)]))
+                elif n >= LAG:
+                    earlier = dict(zip(MULTIPLY_BEHIND, [(made[n - LAG], jp) for jp in range(2)]))
+                else:
+                    earlier = {}
+                made[n] = patch_group(group, following, earlier)
                 group = following
             quantise_pending()
-            for n in range(last - LAG + 1, last):
-                for jp in range(2):
-                    multiply(made[n], jp)
             multiply_last(made[last])

@@ -260,7 +260,7 @@ def tile_shiftedpatchtokenization_pb_t_kernel(tc, x, ln2_g, ln2_b, w2_words, w2_
                 rows_from_above(f)
 
             tensor_steps = [tensor_step(l) for l in TENSOR_PLANES[f]]
-            return tensor_steps[0:1] + [vector_step] + tensor_steps[1:] + [exchange_step] + square_sums_steps(f)
+            return tensor_steps + [vector_step, exchange_step] + square_sums_steps(f)
 
         def load_by_halves(f):
             tiles = []
@@ -394,11 +394,18 @@ def tile_shiftedpatchtokenization_pb_t_kernel(tc, x, ln2_g, ln2_b, w2_words, w2_
                 uv[:, :, :, 0, :], region_sets[f % 2][:, :, 4:12, x0 + 4 : x0 + 12].rearrange("p l a b -> p a b l"),
                 stats[f], j, on_vector,
             )
-            for sy, band in enumerate((upper, lower)):
-                for sx in range(2):
+            for sx in range(2):
+                if on_vector:
+                    for sy, band in enumerate((upper, lower)):
+                        normalise(
+                            uv[:, :, :, 1 + 2 * sy + sx, :],
+                            band[:, :, :, x0 + 8 * sx : x0 + 8 * sx + 8].rearrange("p l a b -> p a b l"),
+                            stats[f], j, on_vector,
+                        )
+                else:
                     normalise(
-                        uv[:, :, :, 1 + 2 * sy + sx, :],
-                        band[:, :, :, x0 + 8 * sx : x0 + 8 * sx + 8].rearrange("p l a b -> p a b l"),
+                        uv[:, :, :, 1 + sx : 5 : 2, :].rearrange("p a b s l -> p s a b l"),
+                        region_sets[f % 2][:, :, :, x0 + 8 * sx : x0 + 8 * sx + 8].rearrange("p l (s a) b -> p s a b l", s=2),
                         stats[f], j, on_vector,
                     )
 

from contextlib import ExitStack

import concourse.mybir as mybir
from concourse.masks import make_identity

F32 = mybir.dt.float32
BF16 = mybir.dt.bfloat16
U32 = mybir.dt.uint32
U8 = mybir.dt.uint8
I32 = mybir.dt.int32
FP8X4 = mybir.dt.float8_e4m3fn_x4
ALU = mybir.AluOpType
ACT = mybir.ActivationFunctionType

P = 128
BATCH = 16
DIM = 512
K = 2560
PASSES = K // 512
EPS = 1e-5
PHASES = 4
IMAGES = BATCH // PHASES
STRIPS = 16
SHIFT = P // STRIPS
PLANES = 4
BAND_ROWS = 8
PADDED = 136
QUAD_PITCH = 34
GROUP = 4
GROUPS = 16 // GROUP
WORDS = K // 2
VECTOR_PATCHES = ((2, 1), (2, 1), (2, 1), (3, 3))
FIRST_VECTOR_PATCHES = 3
TENSOR_PLANES = ((1, 3), (1, 3), (1, 3), (1, 2, 3))
SUMS_BEHIND = 1
STATS_AT = (2, 3)
COPY_UNITS = ((0, 1), (2, 3), (4,))
MULTIPLY_BEHIND = (2, 4)
LAG = 2
CATCH_UP_BEHIND = (1, 2, 3, 4)

FLOPS = 2 * BATCH * 256 * K * DIM


def tile_shiftedpatchtokenization_pb_t_kernel(tc, x, ln2_g, ln2_b, w2_words, w2_scales, b2, tok, out):
    nc = tc.nc
    with ExitStack() as ctx:
        const = ctx.enter_context(tc.tile_pool(name="const", bufs=1))
        x_pool = ctx.enter_context(tc.tile_pool(name="x_pool", bufs=4))
        haar_pool = ctx.enter_context(tc.tile_pool(name="haar_pool", bufs=2))
        stat_pool = ctx.enter_context(tc.tile_pool(name="stat_pool", bufs=2))
        u_pool = ctx.enter_context(tc.tile_pool(name="u_pool", bufs=2))
        z_pool = ctx.enter_context(tc.tile_pool(name="z_pool", bufs=3))
        code_pool = ctx.enter_context(tc.tile_pool(name="code_pool", bufs=3))
        io_pool = ctx.enter_context(tc.tile_pool(name="io_pool", bufs=3))
        tok_pool = ctx.enter_context(tc.tile_pool(name="tok_pool", bufs=6))
        psum_t = ctx.enter_context(tc.psum_pool(name="psum_t", bufs=5))
        psum_mx = ctx.enter_context(tc.psum_pool(name="psum_mx", bufs=3))

        x_rows = x.rearrange("(f b) k (s r) w -> f k s b (r w)", f=PHASES, s=STRIPS)
        tok_rows = tok.rearrange("b t n -> (b t) n").rearrange("(f m j) n -> f m j n", f=PHASES, j=16)
        out_rows = out.rearrange("b t n -> (b t) n").rearrange("(f m j) n -> f m j n", f=PHASES, j=16)

        one = const.tile([P, 1], F32)
        zero = const.tile([P, 1], F32)
        root = const.tile([P, 1], F32)
        nc.gpsimd.memset(one[:], 1.0)
        nc.gpsimd.memset(zero[:], 0.0)
        nc.scalar.activation(out=root[:], in_=one[:], func=ACT.Sqrt)

        band_sets = []
        region_sets = []
        quad_sets = []
        for half in range(2):
            region = const.tile([P, PLANES, 2 * BAND_ROWS, PADDED], F32, name="region%d" % half)
            quads = const.tile([P, 2, 2, QUAD_PITCH], F32, name="quads%d" % half)
            band_sets.append((region[:, :, 0:BAND_ROWS, :], region[:, :, BAND_ROWS : 2 * BAND_ROWS, :]))
            region_sets.append(region)
            quad_sets.append(quads)

        def clear_set(half):
            upper, lower = band_sets[half]
            nc.scalar.copy(out=upper[:, :, 0:4, :], in_=zero[:, 0:1].to_broadcast([P, PLANES, 4, PADDED]))
            nc.scalar.copy(out=lower[:, :, 4:8, :], in_=zero[:, 0:1].to_broadcast([P, PLANES, 4, PADDED]))
            for own in (upper[:, :, 4:8, :], lower[:, :, 0:4, :]):
                nc.vector.memset(own[:, :, :, 0:4], 0.0)
                nc.vector.memset(own[:, :, :, PADDED - 4 : PADDED], 0.0)
            nc.vector.memset(quad_sets[half][:], 0.0)

        clear_set(0)

        ident = const.tile([P, P], F32)
        make_identity(nc, ident[:])
        perm = const.tile([P, P], F32)
        nc.vector.tensor_copy(
            out=perm[:].rearrange("p (c b s) -> p c b s", c=2, b=IMAGES, s=STRIPS),
            in_=ident[:].rearrange("p (s b c) -> p c b s", c=2, b=IMAGES, s=STRIPS),
        )
        pair = const.tile([P, P], F32)
        pair_kc = pair[:].rearrange("p (k c) -> p k c", c=2)
        ident_kc = ident[:].rearrange("p (k c) -> p k c", c=2)
        nc.vector.tensor_copy(out=pair_kc[:, :, 0], in_=ident_kc[:, :, 1])
        nc.vector.tensor_copy(out=pair_kc[:, :, 1], in_=ident_kc[:, :, 0])
        nc.vector.tensor_tensor(out=pair[:], in0=pair[:], in1=ident[:], op=ALU.add)
        from_above = const.tile([P, P], F32)
        from_below = const.tile([P, P], F32)
        nc.vector.memset(from_above[:, 0:SHIFT], 0.0)
        nc.vector.tensor_copy(out=from_above[:, SHIFT:P], in_=pair[:, 0 : P - SHIFT])
        nc.vector.memset(from_below[:, P - SHIFT : P], 0.0)
        nc.vector.tensor_copy(out=from_below[:, 0 : P - SHIFT], in_=pair[:, SHIFT:P])

        three_eye = const.tile([P, P], BF16)
        minus_eye = const.tile([P, P], BF16)
        eye = const.tile([P, P], BF16)
        nc.vector.tensor_copy(out=eye[:], in_=ident[:])
        nc.vector.tensor_scalar(out=three_eye[:], in0=ident[:], scalar1=3.0, scalar2=None, op0=ALU.mult)
        nc.vector.tensor_scalar(out=minus_eye[:], in0=ident[:], scalar1=-1.0, scalar2=None, op0=ALU.mult)

        gain_bf = const.tile([P, PASSES, 4], BF16)
        bias_bf = const.tile([P, PASSES, 4], BF16)
        gain = const.tile([P, PASSES, 4], F32)
        bias = const.tile([P, PASSES, 4], F32)

        w_codes = const.tile([P, PASSES, DIM], U32, align_bytes=64)
        w_scales = const.tile([P, PASSES, DIM], U8, align_bytes=64)
        b2_all = const.tile([P, DIM], BF16)

        def load_weights():
            nc.sync.dma_start(out=gain_bf[:], in_=ln2_g.rearrange("(g p t) -> p g t", g=PASSES, p=P, t=4))
            nc.sync.dma_start(out=bias_bf[:], in_=ln2_b.rearrange("(g p t) -> p g t", g=PASSES, p=P, t=4))
            nc.vector.tensor_copy(out=gain[:], in_=gain_bf[:])
            nc.vector.tensor_copy(out=bias[:], in_=bias_bf[:])
            nc.vector.memset(w_scales[:].bitcast(I32), 0)
            for quadrant in range(4):
                nc.sync.dma_start(
                    out=w_scales[32 * quadrant : 32 * quadrant + 4, :, :].bitcast(I32),
                    in_=w2_scales[:, 4 * quadrant : 4 * quadrant + 4, :].rearrange("g r n -> r g n").bitcast(I32),
                )
            nc.sync.dma_start(
                out=w_codes[:].bitcast(I32),
                in_=w2_words.rearrange("g p n t -> p g (n t)").bitcast(I32),
            )
            nc.sync.dma_start(out=b2_all[:], in_=b2.partition_broadcast(P))

        def load_rows(xt, f, l, first, count):
            for c in range(2):
                nc.sync.dma_start(
                    out=xt[c:P:2, first : first + count, :].rearrange("p r w -> p (r w)"),
                    in_=x_rows[f, 2 * l + c, :, :, first * 256 : (first + count) * 256],
                )

        def as_blocks(xt):
            return xt[:].rearrange("p (r v) (w h) -> p r v w h", v=2, h=2)

        def detail_on_vector(jobs):
            rests = []
            for blocks, dests in jobs:
                rest_tile = haar_pool.tile([P, BAND_ROWS, 128], F32, name="rest")
                rests.append(rest_tile[:, 0 : blocks.shape[1], :])
            for (blocks, dests), rest in zip(jobs, rests):
                nc.vector.tensor_tensor(out=rest, in0=blocks[:, :, 1, :, 0], in1=blocks[:, :, 1, :, 1], op=ALU.add)
            for (blocks, dests), rest in zip(jobs, rests):
                nc.vector.tensor_tensor(out=rest, in0=rest, in1=blocks[:, :, 0, :, 1], op=ALU.add)
            for (blocks, dests), rest in zip(jobs, rests):
                for dest, r0, count in dests:
                    nc.vector.scalar_tensor_tensor(
                        out=dest, in0=blocks[:, r0 : r0 + count, 0, :, 0], scalar=3.0, in1=rest[:, r0 : r0 + count, :],
                        op0=ALU.mult, op1=ALU.subtract,
                    )

        def rest_on_tensor(blocks, r0, dest):
            rest = psum_t.tile([P, 4, P], F32, name="turned")
            for step, (v, h) in enumerate(((0, 1), (1, 0), (1, 1))):
                nc.tensor.matmul(
                    out=rest[:], lhsT=eye[:], rhs=blocks[:, r0 : r0 + 4, v, :, h], start=(step == 0), stop=(step == 2)
                )
            nc.vector.scalar_tensor_tensor(
                out=dest, in0=blocks[:, r0 : r0 + 4, 0, :, 0], scalar=3.0, in1=rest[:], op0=ALU.mult, op1=ALU.subtract
            )

        def detail_on_tensor(blocks, r0, dest):
            detail = psum_t.tile([P, 4, P], F32, name="turned")
            for step, (v, h) in enumerate(((0, 0), (0, 1), (1, 0), (1, 1))):
                nc.tensor.matmul(
                    out=detail[:],
                    lhsT=(three_eye if step == 0 else minus_eye)[:],
                    rhs=blocks[:, r0 : r0 + 4, v, :, h],
                    start=(step == 0),
                    stop=(step == 3),
                )
            nc.scalar.copy(out=dest, in_=detail[:])

        def own_rows(f, l):
            upper, lower = band_sets[f % 2]
            return upper[:, l, 4:8, 4 : PADDED - 4], lower[:, l, 0:4, 4 : PADDED - 4]

        def square_sums_steps(f):
            upper, lower = band_sets[f % 2]
            quads = quad_sets[f % 2]
            halves = ((upper, 4), (lower, 0))
            bn = stat_pool.tile([P, 2, 16, 6], F32, name="bn")

            def count(yq, first):
                band, row = halves[yq]
                for xp in range(first, first + 8):
                    nc.vector.bn_stats(
                        out=bn[:, yq, xp, :],
                        in_=band[:, :, row : row + 4, 4 + 8 * xp : 12 + 8 * xp].rearrange(
                            "p l r (c s) -> p l r s c", c=2
                        ),
                    )

            def count_and_file():
                count(1, 8)
                squares = stat_pool.tile([P, 2, 16, 2], F32, name="squares")
                nc.vector.tensor_tensor(out=squares[:], in0=bn[:, :, :, 1:6:3], in1=bn[:, :, :, 1:6:3], op=ALU.mult)
                nc.vector.tensor_copy(
                    out=quads[:, 0, :, 1:33].rearrange("p y (x c) -> p y x c", c=2), in_=bn[:, :, :, 1:6:3]
                )
                nc.vector.scalar_tensor_tensor(
                    out=quads[:, 1, :, 1:33].rearrange("p y (x c) -> p y x c", c=2),
                    in0=squares[:], scalar=64.0, in1=bn[:, :, :, 2:6:3], op0=ALU.mult, op1=ALU.add,
                )

            return [lambda: count(0, 0), lambda: count(0, 8), lambda: count(1, 0), count_and_file]

        def rows_from_below(f):
            upper, lower = band_sets[f % 2]
            nc.sync.dma_start(out=lower[0 : P - SHIFT, :, 4:8, :], in_=upper[SHIFT:P, :, 4:8, :])

        def rows_from_above(f):
            upper, lower = band_sets[f % 2]
            nc.sync.dma_start(out=upper[SHIFT:P, :, 0:4, :], in_=lower[0 : P - SHIFT, :, 0:4, :])

        def haar_steps(f):
            blocks = []
            for l in range(PLANES):
                xt = x_pool.tile([P, 2 * BAND_ROWS, 256], BF16, name="xt")
                load_rows(xt, f, l, 0, 2 * BAND_ROWS)
                blocks.append(as_blocks(xt))

            def tensor_step(l):
                def make():
                    top, bottom = own_rows(f, l)
                    rest_on_tensor(blocks[l], 0, top)
                    rest_on_tensor(blocks[l], 4, bottom)

                return make

            def vector_step():
                jobs = []
                for l in range(PLANES):
                    if l not in TENSOR_PLANES[f]:
                        own = region_sets[f % 2][:, l, 4:12, 4 : PADDED - 4]
                        jobs.append((blocks[l], ((own, 0, BAND_ROWS),)))
                detail_on_vector(jobs)

            def exchange_step():
                rows_from_below(f)
                rows_from_above(f)

            tensor_steps = [tensor_step(l) for l in TENSOR_PLANES[f]]
            return tensor_steps + [vector_step, exchange_step] + square_sums_steps(f)

        def load_by_halves(f):
            tiles = []
            for l in range(PLANES):
                xt = x_pool.tile([P, 2 * BAND_ROWS, 256], BF16, name="xt")
                tiles.append(xt)
            order = [l for l in range(PLANES) if l not in TENSOR_PLANES[f]] + list(TENSOR_PLANES[f])
            for half in range(2):
                for l in order:
                    load_rows(tiles[l], f, l, 8 * half, 8)
            return tiles

        def haar_by_halves(f, tiles):
            sums = square_sums_steps(f)
            for half in range(2):
                jobs = []
                for l in range(PLANES):
                    blocks = as_blocks(tiles[l])
                    dest = own_rows(f, l)[half]
                    if l in TENSOR_PLANES[f]:
                        detail_on_tensor(blocks, 4 * half, dest)
                    else:
                        jobs.append((blocks[:, 4 * half : 4 * half + 4], ((dest, 0, 4),)))
                detail_on_vector(jobs)
                if half == 0:
                    rows_from_below(f)
                else:
                    rows_from_above(f)
                sums[2 * half]()
                sums[2 * half + 1]()

        def token_sums(f):
            quads = quad_sets[f % 2]
            middle = stat_pool.tile([P, 2, 2, 16], F32, name="middle")
            wide = stat_pool.tile([P, 2, 2, 16], F32, name="wide")
            twice = stat_pool.tile([P, 2, 2, 16], F32, name="twice")
            nc.vector.tensor_tensor(out=middle[:], in0=quads[:, :, :, 1:33:2], in1=quads[:, :, :, 2:34:2], op=ALU.add)
            nc.vector.tensor_tensor(out=wide[:], in0=quads[:, :, :, 0:32:2], in1=quads[:, :, :, 3:34:2], op=ALU.add)
            nc.vector.tensor_tensor(out=wide[:], in0=wide[:], in1=middle[:], op=ALU.add)
            nc.vector.tensor_tensor(out=twice[:], in0=wide[:], in1=middle[:], op=ALU.add)
            own = stat_pool.tile([P, 2, 16], F32, name="own")
            nc.vector.tensor_tensor(out=own[:], in0=twice[:, :, 0, :], in1=twice[:, :, 1, :], op=ALU.add)
            return wide, own

        def token_stats(sums):
            wide, own = sums
            both = psum_t.tile([P, 2, 16], F32, name="turned")
            terms = ((from_above, wide[:, :, 1, :]), (from_below, wide[:, :, 0, :]), (pair, own[:]))
            for step, (giver, part) in enumerate(terms):
                nc.tensor.matmul(out=both[:], lhsT=giver[:], rhs=part, start=(step == 0), stop=(step == len(terms) - 1))
            mean = stat_pool.tile([P, 16], F32, name="mean")
            var = stat_pool.tile([P, 16], F32, name="var")
            minus_sq = stat_pool.tile([P, 16], F32, name="minus_sq")
            std = stat_pool.tile([P, 16], F32, name="std")
            rstd = stat_pool.tile([P, 16], F32, name="rstd")
            shift = stat_pool.tile([P, 16], F32, name="shift")
            nc.vector.tensor_scalar(out=mean[:], in0=both[:, 0, :], scalar1=64.0 / K, scalar2=None, op0=ALU.mult)
            nc.vector.scalar_tensor_tensor(
                out=minus_sq[:], in0=mean[:], scalar=-1.0, in1=mean[:], op0=ALU.mult, op1=ALU.mult
            )
            nc.vector.scalar_tensor_tensor(
                out=var[:], in0=both[:, 1, :], scalar=1.0 / K, in1=minus_sq[:], op0=ALU.mult, op1=ALU.add
            )
            nc.scalar.activation(out=std[:], in_=var[:], func=ACT.Sqrt, bias=36.0 * EPS)
            nc.vector.reciprocal(out=rstd[:], in_=std[:])
            nc.vector.scalar_tensor_tensor(
                out=shift[:], in0=mean[:], scalar=-1.0, in1=rstd[:], op0=ALU.mult, op1=ALU.mult
            )
            return mean, rstd, shift

        def normalise(dst, src, stats, j, on_vector):
            mean, rstd, shift = stats
            if on_vector:
                nc.vector.tensor_scalar(
                    out=dst, in0=src, scalar1=mean[:, j : j + 1], scalar2=rstd[:, j : j + 1],
                    op0=ALU.subtract, op1=ALU.mult,
                )
            else:
                nc.scalar.activation(
                    out=dst, in_=src, func=ACT.Identity, bias=shift[:, j : j + 1], scale=rstd[:, j : j + 1]
                )

        def multiply_pass(group, jp, g, acc):
            cols = slice(P * jp, P * jp + P)
            nc.tensor.matmul_mx(
                out=acc[:],
                lhsT=group["codes"][:, g, cols].bitcast(FP8X4),
                lhsT_scale=group["scales"][:, g, cols],
                rhs=w_codes[:, g, :].bitcast(FP8X4),
                rhs_scale=w_scales[:, g, :],
                start=(g == 0),
                stop=(g == PASSES - 1),
            )

        def add_and_store(group, jp, acc):
            j0 = group["j0"] + 2 * jp
            result = io_pool.tile([P, DIM], F32, name="result")
            nc.vector.tensor_tensor(out=result[:], in0=acc[:], in1=group["tok"][jp][:], op=ALU.add)
            nc.sync.dma_start(out=out_rows[group["f"], :, j0 : j0 + 2, :], in_=result[:])

        def multiply(group, jp):
            acc = psum_mx.tile([P, DIM], F32, name="acc")
            for g in range(PASSES):
                multiply_pass(group, jp, g, acc)
            add_and_store(group, jp, acc)

        def multiply_last(group):
            accs = []
            for jp in range(2):
                acc = psum_mx.tile([P, DIM], F32, name="acc")
                accs.append(acc)
            for g in range(PASSES):
                for jp in range(2):
                    multiply_pass(group, jp, g, accs[jp])
            for jp in range(2):
                add_and_store(group, jp, accs[jp])

        def open_group(n):
            f, jc = divmod(n, GROUPS)
            u = u_pool.tile([P, GROUP, WORDS], F32, name="u")
            return {"n": n, "f": f, "jc": jc, "u": u, "vector_patches": FIRST_VECTOR_PATCHES if n == 0 else VECTOR_PATCHES[f][n % 2]}

        def fill_patch(group, jl):
            f = group["f"]
            upper, lower = band_sets[f % 2]
            j = GROUP * group["jc"] + jl
            on_vector = jl >= GROUP - group["vector_patches"]
            uv = group["u"][:, jl, :].rearrange("p (a b c l) -> p a b c l", a=8, b=8, c=5, l=PLANES)
            x0 = 8 * j
            normalise(
                uv[:, :, :, 0, :], region_sets[f % 2][:, :, 4:12, x0 + 4 : x0 + 12].rearrange("p l a b -> p a b l"),
                stats[f], j, on_vector,
            )
            for sx in range(2):
                if on_vector:
                    for sy, band in enumerate((upper, lower)):
                        normalise(
                            uv[:, :, :, 1 + 2 * sy + sx, :],
                            band[:, :, :, x0 + 8 * sx : x0 + 8 * sx + 8].rearrange("p l a b -> p a b l"),
                            stats[f], j, on_vector,
                        )
                else:
                    normalise(
                        uv[:, :, :, 1 + sx : 5 : 2, :].rearrange("p a b s l -> p s a b l"),
                        region_sets[f % 2][:, :, :, x0 + 8 * sx : x0 + 8 * sx + 8].rearrange("p l (s a) b -> p s a b l", s=2),
                        stats[f], j, on_vector,
                    )

        pending = []

        def quantise_pending():
            for z_codes, z_scales, passes, grouped, count in pending:
                nc.vector.quantize_mx(
                    out=z_codes[:, passes, :].rearrange("p g c -> p (g c)").bitcast(FP8X4),
                    scales=z_scales[:, passes, :].rearrange("p g c -> p (g c)"),
                    in_=grouped[:, 0 : count * 4 * GROUP * 64],
                )
            pending.clear()

        def patch_group(group, following, earlier):
            f = group["f"]
            jc = group["jc"]
            u = group["u"]
            tok_tiles = []
            for jp in range(2):
                j0 = GROUP * jc + 2 * jp
                tok_bf = io_pool.tile([P, DIM], BF16, name="tok_bf")
                nc.sync.dma_start(out=tok_bf[:], in_=tok_rows[f, :, j0 : j0 + 2, :])
                tok_b2 = tok_pool.tile([P, DIM], F32, name="tok_b2")
                nc.gpsimd.tensor_tensor(out=tok_b2[:], in0=tok_bf[:], in1=b2_all[:], op=ALU.add)
                tok_tiles.append(tok_b2)

            z_codes = code_pool.tile([P, PASSES, GROUP * 64], U32, name="z_codes", align_bytes=64)
            z_scales = code_pool.tile([P, PASSES, GROUP * 64], U8, name="z_scales", align_bytes=64)
            for unit in COPY_UNITS:
                count = len(unit)
                planes = z_pool.tile([P, 4, 2 * GROUP * 64], BF16, name="planes")
                for slot, g in enumerate(unit):
                    step = todo.get((group["n"], g))
                    if step is not None:
                        step()
                    if following is not None and g < GROUP:
                        fill_patch(following, g)
                    for ca in range(2):
                        turned = psum_t.tile([P, GROUP, P], F32, name="turned")
                        for jl in range(GROUP):
                            nc.tensor.transpose(
                                out=turned[:, jl, :], in_=u[:, jl, 256 * g + ca : 256 * (g + 1) : 2], identity=perm[:]
                            )
                        for cb in range(2):
                            t = 2 * ca + cb
                            nc.scalar.activation(
                                out=planes[:, t, GROUP * 64 * slot : GROUP * 64 * (slot + 1)].rearrange(
                                    "p (jp m jj) -> p jp m jj", jp=2, m=64, jj=2
                                ),
                                in_=turned[:, :, 64 * cb : 64 * cb + 64].rearrange("p (jp jj) m -> p jp m jj", jj=2),
                                func=ACT.Identity,
                                bias=bias[:, g, t : t + 1],
                                scale=gain[:, g, t : t + 1],
                            )
                    if g in earlier:
                        multiply(*earlier[g])
                passes = slice(unit[0], unit[0] + count)
                grouped = z_pool.tile([P, 2 * 4 * GROUP * 64], BF16, name="grouped", align_bytes=64)
                nc.vector.tensor_copy(
                    out=grouped[:, 0 : count * 4 * GROUP * 64].rearrange("p (c i t) -> p c t i", i=4, t=4),
                    in_=planes[:, :, 0 : count * GROUP * 64].rearrange("p t (c i) -> p c t i", i=4),
                )
                quantise_pending()
                pending.append((z_codes, z_scales, passes, grouped, count))

            return {"codes": z_codes, "scales": z_scales, "tok": tok_tiles, "f": f, "j0": GROUP * jc}

        stats = {}
        row_sums = {}
        todo = {}

        def sums_step(f):
            def make():
                row_sums[f] = token_sums(f)

            return make

        def stats_step(f):
            def make():
                stats[f] = token_stats(row_sums[f])

            return make

        with tc.manual_schedule(engines={mybir.EngineType.PE}):
            first_tiles = load_by_halves(0)
            load_weights()
            haar_by_halves(0, first_tiles)
            clear_set(1)
            stats[0] = token_stats(token_sums(0))
            group = open_group(0)
            for jl in range(GROUP):
                fill_patch(group, jl)
            made = {}
            last = PHASES * GROUPS - 1
            for n in range(PHASES * GROUPS):
                f, jc = divmod(n, GROUPS)
                if jc == 0 and f + 1 < PHASES:
                    steps = haar_steps(f + 1)
                    for k, step in enumerate(steps):
                        todo[(n + k // PASSES, k % PASSES)] = step
                    k = len(steps) - 1 + SUMS_BEHIND
                    todo[(n + k // PASSES, k % PASSES)] = sums_step(f + 1)
                    todo[(n + STATS_AT[0], STATS_AT[1])] = stats_step(f + 1)
                following = open_group(n + 1) if n + 1 < PHASES * GROUPS else None
                if n == last:
                    earlier = dict(zip(CATCH_UP_BEHIND, [(made[m], jp) for m in range(last - LAG, last) for jp in range(2)]))
                elif n >= LAG:
                    earlier = dict(zip(MULTIPLY_BEHIND, [(made[n - LAG], jp) for jp in range(2)]))
                else:
                    earlier = {}
                made[n] = patch_group(group, following, earlier)
                group = following
            quantise_pending()
            multiply_last(made[last])
